import numpy as np
import ml_dtypes


def mxq(x, axis, fmt="e4m3"):
    dtype, down = {"e4m3": (ml_dtypes.float8_e4m3fn, 7), "e5m2": (ml_dtypes.float8_e5m2, 14)}[fmt]
    v = np.moveaxis(np.asarray(x, np.float32).astype(ml_dtypes.bfloat16).astype(np.float64), axis, -1)
    blocks = v.reshape(v.shape[:-1] + (-1, 32))
    amax = np.abs(blocks).max(-1, keepdims=True)
    byte = np.maximum(np.where(amax > 0, np.frexp(amax)[1] - 1 + 127, 0) - down, 1)
    scale = np.exp2(byte - 127.0)
    codes = (blocks / scale).astype(np.float32).astype(dtype).astype(np.float64)
    return np.moveaxis((codes * scale).reshape(v.shape), -1, axis)


WIDE = False


def mx_kscale(k):
    if not WIDE:
        return np.ones(k)
    levels = np.array([10, -10, 5, -5, 0])
    a = np.random.permutation(np.resize(levels, k // 512 * 4)).reshape(k // 512, 4)
    idx = np.arange(k)
    return np.exp2(a[idx // 512, idx % 128 // 32])


BF16 = ml_dtypes.bfloat16


def bf(x):
    return np.asarray(x, np.float32).astype(BF16)


def f64(x):
    return np.asarray(x).astype(np.float64)


E2M1 = np.array([0.0, 0.5, 1.0, 1.5, 2.0, 3.0, 4.0, 6.0, -0.0, -0.5, -1.0, -1.5, -2.0, -3.0, -4.0, -6.0])


def pack_weight(w, fmt):
    k, n = w.shape
    w = f64(bf(w)).reshape(k // 32, 32, n)
    amax = np.abs(w).max(1)
    if fmt == "e4m3":
        byte = np.frexp(amax)[1] - 1 + 127 - 7
    else:
        mant, ex = np.frexp(amax / 6.0)
        byte = np.where(mant > 0.5, ex, ex - 1) + 127
    byte = np.clip(np.where(amax > 0, byte, 1), 1, 254)
    scaled = (w * np.exp2(127.0 - byte)[:, None, :]).reshape(k, n).astype(np.float32)
    by_word = np.ascontiguousarray(scaled.reshape(k // 512, 128, 4, n).transpose(0, 1, 3, 2))
    if fmt == "e4m3":
        words = by_word.astype(ml_dtypes.float8_e4m3fn).view(np.uint8)
    else:
        c = by_word.astype(ml_dtypes.float4_e2m1fn).view(np.uint8) & 0xF
        words = c[..., 0::2] | (c[..., 1::2] << 4)
    return np.ascontiguousarray(words), np.ascontiguousarray(byte.astype(np.uint8).reshape(k // 512, 16, n))


def unpack_weight(words, scales, fmt):
    g, p, n, _ = words.shape
    if fmt == "e4m3":
        vals = np.ascontiguousarray(words).view(ml_dtypes.float8_e4m3fn).astype(np.float64)
    else:
        nib = np.empty((g, p, n, 4), np.uint8)
        nib[..., 0::2] = words & 0xF
        nib[..., 1::2] = words >> 4
        vals = E2M1[nib]
    vals = vals * np.repeat(np.exp2(scales.astype(np.float64) - 127.0), 8, axis=1)[..., None]
    return vals.transpose(0, 1, 3, 2).reshape(g * 512, n)

def pack4(w):
    words, scales = pack_weight(w, "e2m1")
    return words.reshape(words.shape[0], 128, -1), scales


def unpack4(words, scales):
    return unpack_weight(words.reshape(words.shape[0], 128, -1, 2), scales, "e2m1")


B, IN, OUT, CHEBY_ORDER = 1024, 512, 512, 10


def silu(v):
    return v / (1.0 + np.exp(-v))


def chebyshev_bases(x, order):
    t0 = np.ones_like(x)
    if order == 1:
        return t0[None]
    ts = [t0, x]
    for _ in range(2, order):
        ts.append(2.0 * x * ts[-1] - ts[-2])
    return np.stack(ts)


def setup_inputs():
    u = np.minimum(mx_kscale(IN), 1.0) ** 2
    x = bf(np.random.random_sample((B, IN)) * u)
    base_weight = np.random.standard_normal((OUT, IN)) * 0.05 / u
    words, scales = pack4(np.ascontiguousarray(base_weight.T))
    cheby_weight = bf(np.random.standard_normal((OUT, IN, CHEBY_ORDER)) * 0.05)
    return {"x": x,
            "base_weight_words": words,
            "base_weight_scales": scales,
            "cheby_weight": cheby_weight}


def reference(x, base_weight_words, base_weight_scales, cheby_weight):
    x = f64(x)
    cheby_weight = f64(cheby_weight)
    b, n_in = x.shape
    n_out, _, o = cheby_weight.shape
    base_out = mxq(silu(x), 1, "e4m3") @ unpack4(base_weight_words, base_weight_scales)
    bases = chebyshev_bases(x, o)
    flat = bases.reshape(b, o * n_in)
    w = cheby_weight.reshape(n_out, n_in * o)
    spline_out = (mxq(flat, 1, "e4m3") @ mxq(w, 1, "e4m3").T) / o
    return base_out + spline_out

@@ -1,0 +1,316 @@
+from contextlib import ExitStack
+
+import concourse.mybir as mybir
+from concourse.masks import make_identity
+
+F32 = mybir.dt.float32
+BF16 = mybir.dt.bfloat16
+I32 = mybir.dt.int32
+U32 = mybir.dt.uint32
+U8 = mybir.dt.uint8
+FP8X4 = mybir.dt.float8_e4m3fn_x4
+FP4X4 = mybir.dt.float4_e2m1fn_x4
+ALU = mybir.AluOpType
+ACT = mybir.ActivationFunctionType
+
+P = 128
+B = 1024
+IN = 512
+OUT = 512
+ORD = 10
+NB = 104
+CW = NB * 4
+FTW = 2048 + 32
+
+FLOPS = 2 * B * OUT * (IN + IN * ORD)
+
+ORDER = (
+    "wd0", "wd1", "tx0", "tx1", "ex0", "tx2", "ex1", "F0", "tx3", "ex2", "F1", "tx4", "T1_0", "wd2",
+    "ex3", "F2", "ex4", "T1_1", "F3", "tw0_0", "t3a", "tw1_0", "F4", "tw0_1", "ew0_0", "ew1_0", "t3b",
+    "Hb", "tw2_1", "tw1_1", "wd3", "ew0_1", "ew2_1", "T2_1", "tw2_0", "ew1_1", "Ha", "tw3_0", "tw4_0",
+    "ew2_0", "qw0", "tw3_1", "T2_0", "G2b", "wd4", "q0_0", "qw2", "qw1", "ew3_1", "q0_1", "T3_1", "T5_0",
+    "G2a", "ew4_0", "ew3_0", "tw5_1", "tw4_1", "m7b", "ew5_1", "ew4_1", "T3_0", "tw6_0", "tw5_0", "qw4",
+    "xn", "qw3", "q1_0", "ew5_0", "G3a", "qw5", "tw6_1", "T4_0", "tw7_0", "q1_1", "ew6_0", "ew7_0",
+    "ew6_1", "m7a", "tw8_1", "G3b", "tw7_1", "tw8_0", "p0_0", "ew7_1", "ew8_0", "qw6", "ew8_1", "tw9_0",
+    "qw7", "T6_1", "tw9_1", "T4_1", "tn0", "ew9_0", "si0", "q2_1", "tn1", "p1_0", "ew9_1", "qw8", "si1",
+    "q2_0", "tn3", "qw9", "G4a", "qs0", "T6_0", "bp0", "p2_0", "be0", "T7_1", "tn2", "G4b", "bp1",
+    "p0_1", "be1", "q3_0", "bp2", "p1_1", "be2", "q3_1", "si2", "T7_0", "p2_1", "si3", "q4_0", "p3_0",
+    "T8_1", "q5_1", "q5_0", "T8_0", "bp3", "p3_1", "f1", "qs1", "f2", "p5_0", "f0", "q4_1", "p5_1",
+    "be3", "q6_0", "T9_0", "bp4", "p6_0", "be4", "p4_0", "f3", "q6_1", "bp5", "T9_1", "p4_1", "be5",
+    "bp6", "p6_1", "be6", "q7_0", "f4", "p7_0", "q7_1", "f6", "bp7", "p7_1", "be7", "f5", "f7",
+)
+
+ON_VECTOR = (
+    "ex0", "ex1", "ex2", "ex3", "ex4", "T2_0", "T2_1", "T4_0", "T4_1", "T6_0", "ew0_1", "ew2_0", "ew5_0",
+    "ew7_0", "ew7_1", "ew9_0",
+)
+
+
+def runs_of(n):
+    out = []
+    for rho in range(ORD):
+        s = 4 * n + rho
+        c, m0 = s % ORD, 102 * n + s // ORD
+        if out and out[-1][3] == m0:
+            out[-1][1] = rho + 1
+        else:
+            out.append([rho, rho + 1, c, m0])
+    return out
+
+
+def tile_kantlinear_kernel(tc, x, base_weight_words, base_weight_scales, cheby_weight, out):
+    nc = tc.nc
+    with ExitStack() as ctx:
+        keep = ctx.enter_context(tc.tile_pool(name="keep", bufs=1))
+        ps = ctx.enter_context(tc.psum_pool(name="ps", bufs=1))
+        ctx.enter_context(tc.manual_schedule())
+
+        ident = keep.tile([P, P], F32, name="ident")
+        make_identity(nc, ident[:])
+        ft = keep.tile([P, ORD, FTW], BF16, name="ft", align_bytes=64)
+        nc.gpsimd.memset(ft[:, :, 0:CW], 1.0)
+
+        xs = keep.tile([P, 5120], BF16, name="xs", tag="raw0")
+        xrows = x[0:960, :].rearrange("(b r) i -> b r i", r=ORD)
+        nc.sync.dma_start(out=xs[103:128, :], in_=x[0:250, :].rearrange("(b r) i -> b (r i)", r=ORD))
+        nc.sync.dma_start(out=xs[96:102, :], in_=x[960:1020, :].rearrange("(b r) i -> b (r i)", r=ORD))
+        nc.sync.dma_start(out=xs[102:103, 0:2048], in_=x[1020:1024, :].rearrange("(o r) i -> o (r i)", o=1))
+        nc.sync.dma_start(out=xs[102:103, 2048:5120], in_=x[0:6, :].rearrange("(o r) i -> o (r i)", o=1))
+        for k in range(5):
+            nc.sync.dma_start(
+                out=xs[0:96, k * 1024 : (k + 1) * 1024].rearrange("p (r i) -> p r i", r=2),
+                in_=xrows[:, 2 * k : 2 * k + 2, :],
+            )
+
+        w4 = keep.tile([P, 2 * OUT], U8, name="w4", align_bytes=64)
+        w4s = keep.tile([P, OUT], U8, name="w4s", align_bytes=64)
+        nc.vector.memset(w4s[:].bitcast(I32), 0)
+
+        cw = cheby_weight.rearrange("o i k -> o (i k)")
+
+        xt = keep.tile([P, ORD, CW], BF16, name="xt")
+        ta = keep.tile([P, ORD, CW], F32, name="ta")
+        tb = keep.tile([P, ORD, CW], F32, name="tb")
+        te = keep.tile([P, ORD, CW], F32, name="te")
+        t3 = keep.tile([P, ORD, CW], F32, name="t3")
+
+        w_words = keep.tile([P, ORD, OUT], U32, name="w_words", align_bytes=64)
+        w_scales = keep.tile([P, ORD, OUT], U8, name="w_scales", align_bytes=64)
+        s_words = keep.tile([P, B], U32, name="s_words", align_bytes=64)
+        s_scales = keep.tile([P, B], U8, name="s_scales", align_bytes=64)
+        base_sb = keep.tile([P, 8, OUT], F32, name="base_sb")
+
+        xs_w = xs[:].bitcast(F32)
+        xt_w = xt[:].bitcast(F32)
+        live = {}
+        steps = {}
+
+        def tp_tile(idx, shape):
+            return ps.tile(shape, F32, name="tp_%d" % idx, tag="tp%d" % (idx % 3))
+
+        def copy_on(name, dst, src):
+            if name in ON_VECTOR:
+                nc.vector.tensor_copy(out=dst, in_=src)
+            else:
+                nc.scalar.copy(out=dst, in_=src)
+
+        def tx(k):
+            pt = tp_tile(k, [P, 2, 2, P])
+            live["pt%d" % k] = pt
+            for r in range(2):
+                for u in range(2):
+                    lo = (2 * k + r) * 256 + u * P
+                    nc.tensor.transpose(pt[:, r, u, :], xs_w[:, lo : lo + P], ident[:])
+
+        def ex(k):
+            copy_on(
+                "ex%d" % k,
+                xt_w[:, 2 * k : 2 * k + 2, :].rearrange("p r (b u) -> p r b u", u=2),
+                live["pt%d" % k][:, :, :, 0:NB].rearrange("p r u b -> p r b u"),
+            )
+
+        def sq(dst, src, a, b, scale, bias):
+            nc.scalar.activation(out=dst[:, a:b, :], in_=src[:, a:b, :], func=ACT.Square, bias=bias, scale=scale)
+
+        def stt(dst, in0, scalar, in1):
+            nc.vector.scalar_tensor_tensor(out=dst, in0=in0, scalar=scalar, in1=in1, op0=ALU.add, op1=ALU.mult)
+
+        def fin(n, j):
+            ra, rb, ca, m0 = runs_of(n)[j]
+            mm = m0 % 512
+            dst = ft[:, ca : ca + (rb - ra), 4 * mm : 4 * mm + CW]
+            if n == 1:
+                nc.vector.tensor_copy(out=dst, in_=xt[:, ra:rb, :])
+            elif n in (2, 4, 6, 8):
+                src = {2: ta, 4: tb, 6: ta, 8: tb}[n]
+                if ("T%d_%d" % (n, j)) in ON_VECTOR:
+                    nc.vector.tensor_scalar(
+                        out=dst, in0=src[:, ra:rb, :], scalar1=0.5, scalar2=-1.0, op0=ALU.mult, op1=ALU.add)
+                else:
+                    nc.scalar.activation(out=dst, in_=src[:, ra:rb, :], func=ACT.Copy, bias=-1.0, scale=0.5)
+            elif n == 3:
+                copy_on("T3_%d" % j, dst, t3[:, ra:rb, :])
+            elif n == 5:
+                stt(dst, te[:, ra:rb, :], -1.25, xt[:, ra:rb, :])
+            elif n == 7:
+                nc.vector.tensor_tensor(out=dst, in0=te[:, ra:rb, :], in1=xt[:, ra:rb, :], op=ALU.subtract)
+            else:
+                stt(dst, ta[:, ra:rb, :], -3.0, t3[:, ra:rb, :])
+
+        def wd(g):
+            wr = keep.tile([P, 5120], BF16, name="wr%d" % g, tag="raw%d" % ((g + 1) % 3))
+            live["wr%d" % g] = wr
+            nc.sync.dma_start(
+                out=wr[:, 0:4096].rearrange("p (t j) -> p t j", t=4),
+                in_=cw[:, g * 1024 : (g + 1) * 1024].rearrange("(t o) j -> o t j", o=P),
+            )
+
+        def tw(c, h):
+            pw = tp_tile(5 + 2 * c + h, [P, 2, 2 * P])
+            live["pw%d_%d" % (c, h)] = pw
+            wr_w = live["wr%d" % (c // 2)][:].bitcast(F32)
+            for ol in range(2):
+                for u in range(2):
+                    lo = (2 * h + ol) * 512 + (c % 2) * 256 + u * P
+                    nc.tensor.transpose(pw[:, u, ol * P : (ol + 1) * P], wr_w[:, lo : lo + P], ident[:])
+
+        def ew(c, h):
+            key = "wtg%d" % c
+            if key not in live:
+                live[key] = keep.tile([P, 2048], BF16, name=key, tag="grp%d" % (c % 3), align_bytes=64)
+            wtg_w = live[key][:].bitcast(F32).rearrange("p (o u) -> p o u", u=2)
+            copy_on(
+                "ew%d_%d" % (c, h),
+                wtg_w[:, h * 256 : (h + 1) * 256, :],
+                live["pw%d_%d" % (c, h)][:].rearrange("p u o -> p o u"),
+            )
+
+        def qw(c):
+            nc.vector.quantize_mx(
+                out=w_words[:, c, :].bitcast(FP8X4), scales=w_scales[:, c, :], in_=live["wtg%d" % c][:])
+
+        def xn_load():
+            xn = keep.tile([P, 5120], BF16, name="xn", tag="raw0")
+            live["xn"] = xn
+            nc.sync.dma_start(
+                out=xn[:, 0:4096].rearrange("p (j i) -> p j i", j=8), in_=x.rearrange("(j q) i -> q j i", q=P))
+            nc.sync.dma_start(out=w4[:].bitcast(I32), in_=base_weight_words[0].bitcast(I32))
+            for q in range(4):
+                nc.sync.dma_start(
+                    out=w4s[32 * q : 32 * q + 4, :].bitcast(I32),
+                    in_=base_weight_scales[0, 4 * q : 4 * q + 4, :].bitcast(I32),
+                )
+
+        def tn(k):
+            pn = tp_tile(25 + k, [P, 2, 2 * P])
+            live["pn%d" % k] = pn
+            xn_w = live["xn"][:].bitcast(F32)
+            for jj in range(2):
+                j = 2 * k + jj
+                for u in range(2):
+                    nc.tensor.transpose(
+                        pn[:, u, jj * P : (jj + 1) * P], xn_w[:, j * 256 + u : (j + 1) * 256 : 2], ident[:])
+
+        def si(k):
+            key = "sil%d" % (k // 2)
+            if key not in live:
+                live[key] = keep.tile([P, 2048], BF16, name=key, tag="grp%d" % (1 + k // 2), align_bytes=64)
+            nc.scalar.activation(
+                out=live[key][:, (k % 2) * 1024 : (k % 2 + 1) * 1024].rearrange("p (q u e) -> p q u e", u=2, e=2),
+                in_=live["pn%d" % k][:].bitcast(BF16).rearrange("p u (q e) -> p q u e", e=2),
+                func=ACT.Silu,
+            )
+
+        def qs(h):
+            nc.vector.quantize_mx(
+                out=s_words[:, h * 512 : (h + 1) * 512].bitcast(FP8X4),
+                scales=s_scales[:, h * 512 : (h + 1) * 512],
+                in_=live["sil%d" % h][:],
+            )
+
+        def bp(m):
+            pb = ps.tile([P, OUT], F32, name="pb%d" % m, tag="bb")
+            live["pb%d" % m] = pb
+            nc.tensor.matmul_mx(
+                out=pb[:],
+                lhsT=s_words[:, m * P : (m + 1) * P].bitcast(FP8X4),
+                lhsT_scale=s_scales[:, m * P : (m + 1) * P],
+                rhs=w4[:].bitcast(FP4X4),
+                rhs_scale=w4s[:],
+                start=True,
+                stop=True,
+            )
+
+        def be(m):
+            copy_on("be%d" % m, base_sb[:, m, :], live["pb%d" % m][:])
+
+        def qt(m, h):
+            if ("fw%d" % m) not in live:
+                live["fw%d" % m] = keep.tile([P, ORD, P], U32, name="fw%d" % m, tag="fw%d" % (m % 3), align_bytes=64)
+                live["fs%d" % m] = keep.tile([P, ORD, P], U8, name="fs%d" % m, tag="fs%d" % (m % 3), align_bytes=64)
+            lo = (m % 4) * 512
+            for c in range(5 * h, 5 * h + 5):
+                nc.vector.quantize_mx(
+                    out=live["fw%d" % m][:, c, :].bitcast(FP8X4),
+                    scales=live["fs%d" % m][:, c, :],
+                    in_=ft[:, c, lo : lo + 512],
+                )
+
+        def pt_(m, h):
+            if h == 0:
+                live["acc%d" % m] = ps.tile([P, OUT], F32, name="acc%d" % m, tag="acc%d" % (m % 4))
+            for c in range(5 * h, 5 * h + 5):
+                nc.tensor.matmul_mx(
+                    out=live["acc%d" % m][:],
+                    lhsT=live["fw%d" % m][:, c, :].bitcast(FP8X4),
+                    lhsT_scale=live["fs%d" % m][:, c, :],
+                    rhs=w_words[:, c, :].bitcast(FP8X4),
+                    rhs_scale=w_scales[:, c, :],
+                    start=(c == 0),
+                    stop=(c == ORD - 1),
+                )
+
+        def fo(m):
+            res = keep.tile([P, OUT], F32, name="res%d" % m, tag="res%d" % (m % 3))
+            nc.vector.scalar_tensor_tensor(
+                out=res[:], in0=live["acc%d" % m][:], scalar=0.1, in1=base_sb[:, m, :], op0=ALU.mult, op1=ALU.add)
+            nc.sync.dma_start(out=out[m * P : (m + 1) * P, :], in_=res[:])
+
+        for k in range(5):
+            steps["tx%d" % k] = (tx, (k,))
+            steps["ex%d" % k] = (ex, (k,))
+            steps["F%d" % k] = (sq, (ta, xt, 2 * k, 2 * k + 2, 2.0, 0.0))
+            steps["wd%d" % k] = (wd, (k,))
+        for n in range(1, ORD):
+            for j in range(len(runs_of(n))):
+                steps["T%d_%d" % (n, j)] = (fin, (n, j))
+        for hn, a, b in (("a", 0, 5), ("b", 5, 10)):
+            steps["t3" + hn] = (stt, (t3[:, a:b, :], ta[:, a:b, :], -3.0, xt[:, a:b, :]))
+            steps["G2" + hn] = (sq, (tb, ta, a, b, 1.0, -2.0))
+            steps["H" + hn] = (sq, (te, ta, a, b, 1.0, -2.5))
+            steps["G3" + hn] = (sq, (ta, t3, a, b, 2.0, 0.0))
+            steps["m7" + hn] = (stt, (te[:, a:b, :], tb[:, a:b, :], -2.0, t3[:, a:b, :]))
+            steps["G4" + hn] = (sq, (tb, tb, a, b, 1.0, -2.0))
+        for c in range(ORD):
+            steps["qw%d" % c] = (qw, (c,))
+            for h in range(2):
+                steps["tw%d_%d" % (c, h)] = (tw, (c, h))
+                steps["ew%d_%d" % (c, h)] = (ew, (c, h))
+        steps["xn"] = (xn_load, ())
+        for k in range(4):
+            steps["tn%d" % k] = (tn, (k,))
+            steps["si%d" % k] = (si, (k,))
+        for h in range(2):
+            steps["qs%d" % h] = (qs, (h,))
+        for m in range(8):
+            steps["bp%d" % m] = (bp, (m,))
+            steps["be%d" % m] = (be, (m,))
+            steps["f%d" % m] = (fo, (m,))
+            for h in range(2):
+                steps["q%d_%d" % (m, h)] = (qt, (m, h))
+                steps["p%d_%d" % (m, h)] = (pt_, (m, h))
+
+        assert len(ORDER) == len(steps)
+        for name in ORDER:
+            fn, args = steps[name]
+            fn(*args)

@@ -25,24 +25,24 @@ FTW = 2048 + 32
 FLOPS = 2 * B * OUT * (IN + IN * ORD)
 
 ORDER = (
-    "wd0", "wd1", "tx0", "tx1", "ex0", "tx2", "ex1", "F0", "tx3", "ex2", "F1", "tx4", "T1_0", "wd2",
-    "ex3", "F2", "ex4", "T1_1", "F3", "tw0_0", "t3a", "tw1_0", "F4", "tw0_1", "ew0_0", "ew1_0", "t3b",
-    "Hb", "tw2_1", "tw1_1", "wd3", "ew0_1", "ew2_1", "T2_1", "tw2_0", "ew1_1", "Ha", "tw3_0", "tw4_0",
-    "ew2_0", "qw0", "tw3_1", "T2_0", "G2b", "wd4", "q0_0", "qw2", "qw1", "ew3_1", "q0_1", "T3_1", "T5_0",
-    "G2a", "ew4_0", "ew3_0", "tw5_1", "tw4_1", "m7b", "ew5_1", "ew4_1", "T3_0", "tw6_0", "tw5_0", "qw4",
-    "xn", "qw3", "q1_0", "ew5_0", "G3a", "qw5", "tw6_1", "T4_0", "tw7_0", "q1_1", "ew6_0", "ew7_0",
-    "ew6_1", "m7a", "tw8_1", "G3b", "tw7_1", "tw8_0", "p0_0", "ew7_1", "ew8_0", "qw6", "ew8_1", "tw9_0",
-    "qw7", "T6_1", "tw9_1", "T4_1", "tn0", "ew9_0", "si0", "q2_1", "tn1", "p1_0", "ew9_1", "qw8", "si1",
-    "q2_0", "tn3", "qw9", "G4a", "qs0", "T6_0", "bp0", "p2_0", "be0", "T7_1", "tn2", "G4b", "bp1",
-    "p0_1", "be1", "q3_0", "bp2", "p1_1", "be2", "q3_1", "si2", "T7_0", "p2_1", "si3", "q4_0", "p3_0",
-    "T8_1", "q5_1", "q5_0", "T8_0", "bp3", "p3_1", "f1", "qs1", "f2", "p5_0", "f0", "q4_1", "p5_1",
-    "be3", "q6_0", "T9_0", "bp4", "p6_0", "be4", "p4_0", "f3", "q6_1", "bp5", "T9_1", "p4_1", "be5",
-    "bp6", "p6_1", "be6", "q7_0", "f4", "p7_0", "q7_1", "f6", "bp7", "p7_1", "be7", "f5", "f7",
+    "wd0", "wd1", "tx0", "tx1", "ex0", "tx2", "F0", "ex1", "ex2", "tx4", "F1", "T1_0", "tx3", "ex4",
+    "q0_1", "wd2", "F2", "ex3", "T2_0", "tw0_0", "F4", "T1_1", "tw0_1", "G2a", "ew0_0", "tw1_0", "ew0_1",
+    "tw1_1", "t3a", "tw2_0", "wd3", "ew1_0", "ew1_1", "tw2_1", "F3", "qw0", "tw3_0", "q0_0", "ew2_1",
+    "qw1", "ew3_0", "T2_1", "ew2_0", "Hb", "tw3_1", "tw4_1", "wd4", "q1_0", "tw4_0", "qw2", "ew4_1",
+    "ew3_1", "ew4_0", "tw6_0", "t3b", "Ha", "tw5_1", "tw5_0", "xn", "qw3", "ew5_1", "T3_0", "ew5_0",
+    "ew6_0", "tw6_1", "G2b", "tw7_0", "qw4", "T5_0", "ew6_1", "ew7_0", "tw8_0", "G3a", "tw8_1", "tw7_1",
+    "p1_0", "qw6", "G3b", "T3_1", "q2_0", "ew7_1", "qw5", "tw9_0", "qw7", "ew8_0", "m7b", "ew9_0",
+    "ew8_1", "tn1", "T4_0", "tw9_1", "p0_0", "q1_1", "T6_1", "ew9_1", "tn0", "si1", "q2_1", "p2_0",
+    "qw8", "si0", "qw9", "T4_1", "T6_0", "p1_1", "qs0", "tn2", "m7a", "bp0", "p0_1", "be0", "si2", "tn3",
+    "T7_0", "G4a", "bp1", "q4_0", "f0", "T7_1", "be1", "p4_0", "si3", "bp2", "p2_1", "be2", "G4b", "bp3",
+    "q3_1", "q3_0", "be3", "f2", "p3_0", "T8_0", "f1", "q5_0", "p3_1", "q5_1", "T8_1", "p5_0", "qs1",
+    "q4_1", "bp4", "f3", "be4", "p4_1", "q6_0", "T9_1", "bp5", "p6_0", "be5", "bp6", "p5_1", "be6",
+    "q7_0", "q6_1", "bp7", "p7_0", "be7", "f4", "T9_0", "p6_1", "q7_1", "f5", "p7_1", "f6", "f7",
 )
 
 ON_VECTOR = (
-    "ex0", "ex1", "ex2", "ex3", "ex4", "T2_0", "T2_1", "T4_0", "T4_1", "T6_0", "ew0_1", "ew2_0", "ew5_0",
-    "ew7_0", "ew7_1", "ew9_0",
+    "ex1", "ex2", "ex3", "T2_0", "T2_1", "T3_0", "T3_1", "T4_1", "T6_1", "T8_1", "ew0_0", "ew0_1",
+    "ew3_1", "ew7_1",
 )
 
 
@@ -65,22 +65,33 @@ def tile_kantlinear_kernel(tc, x, base_weight_words, base_weight_scales, cheby_w
         ps = ctx.enter_context(tc.psum_pool(name="ps", bufs=1))
         ctx.enter_context(tc.manual_schedule())
 
+        warm = keep.tile([P, 2], F32, name="warm")
+        nc.vector.memset(warm[:, 0:1], 0.0)
+        nc.scalar.activation(out=warm[:, 1:2], in_=warm[:, 0:1], func=ACT.Silu)
         ident = keep.tile([P, P], F32, name="ident")
         make_identity(nc, ident[:])
         ft = keep.tile([P, ORD, FTW], BF16, name="ft", align_bytes=64)
-        nc.gpsimd.memset(ft[:, :, 0:CW], 1.0)
-
         xs = keep.tile([P, 5120], BF16, name="xs", tag="raw0")
+        nc.vector.memset(xs[96:128, 0:2560].bitcast(F32), 0.0)
+        nc.gpsimd.memset(xs[96:128, 2560:5120].bitcast(F32), 0.0)
+        nc.vector.memset(ft[:, 0:5, 0:CW], 1.0)
+        nc.gpsimd.memset(ft[:, 5:10, 0:CW], 1.0)
+
         xrows = x[0:960, :].rearrange("(b r) i -> b r i", r=ORD)
-        nc.sync.dma_start(out=xs[103:128, :], in_=x[0:250, :].rearrange("(b r) i -> b (r i)", r=ORD))
-        nc.sync.dma_start(out=xs[96:102, :], in_=x[960:1020, :].rearrange("(b r) i -> b (r i)", r=ORD))
+
+        def load_classes(ra, rb):
+            for pa, pb in ((32, 96), (0, 32)):
+                nc.sync.dma_start(
+                    out=xs[pa:pb, ra * 512 : rb * 512].rearrange("p (r i) -> p r i", r=rb - ra),
+                    in_=xrows[pa:pb, ra:rb, :],
+                )
+
+        load_classes(0, 2)
+        nc.sync.dma_start(out=xs[96:100, :], in_=x[960:1000, :].rearrange("(b r) i -> b (r i)", r=ORD))
+        nc.sync.dma_start(out=xs[100:102, :], in_=x[1000:1020, :].rearrange("(b r) i -> b (r i)", r=ORD))
         nc.sync.dma_start(out=xs[102:103, 0:2048], in_=x[1020:1024, :].rearrange("(o r) i -> o (r i)", o=1))
-        nc.sync.dma_start(out=xs[102:103, 2048:5120], in_=x[0:6, :].rearrange("(o r) i -> o (r i)", o=1))
-        for k in range(5):
-            nc.sync.dma_start(
-                out=xs[0:96, k * 1024 : (k + 1) * 1024].rearrange("p (r i) -> p r i", r=2),
-                in_=xrows[:, 2 * k : 2 * k + 2, :],
-            )
+        load_classes(2, 6)
+        load_classes(6, 10)
 
         w4 = keep.tile([P, 2 * OUT], U8, name="w4", align_bytes=64)
         w4s = keep.tile([P, OUT], U8, name="w4s", align_bytes=64)

@@ -25,25 +25,32 @@ FTW = 2048 + 32
 FLOPS = 2 * B * OUT * (IN + IN * ORD)
 
 ORDER = (
-    "wd0", "wd1", "tx0", "tx1", "ex0", "tx2", "F0", "ex1", "ex2", "tx4", "F1", "T1_0", "tx3", "ex4",
-    "q0_1", "wd2", "F2", "ex3", "T2_0", "tw0_0", "F4", "T1_1", "tw0_1", "G2a", "ew0_0", "tw1_0", "ew0_1",
-    "tw1_1", "t3a", "tw2_0", "wd3", "ew1_0", "ew1_1", "tw2_1", "F3", "qw0", "tw3_0", "q0_0", "ew2_1",
-    "qw1", "ew3_0", "T2_1", "ew2_0", "Hb", "tw3_1", "tw4_1", "wd4", "q1_0", "tw4_0", "qw2", "ew4_1",
-    "ew3_1", "ew4_0", "tw6_0", "t3b", "Ha", "tw5_1", "tw5_0", "xn", "qw3", "ew5_1", "T3_0", "ew5_0",
-    "ew6_0", "tw6_1", "G2b", "tw7_0", "qw4", "T5_0", "ew6_1", "ew7_0", "tw8_0", "G3a", "tw8_1", "tw7_1",
-    "p1_0", "qw6", "G3b", "T3_1", "q2_0", "ew7_1", "qw5", "tw9_0", "qw7", "ew8_0", "m7b", "ew9_0",
-    "ew8_1", "tn1", "T4_0", "tw9_1", "p0_0", "q1_1", "T6_1", "ew9_1", "tn0", "si1", "q2_1", "p2_0",
-    "qw8", "si0", "qw9", "T4_1", "T6_0", "p1_1", "qs0", "tn2", "m7a", "bp0", "p0_1", "be0", "si2", "tn3",
-    "T7_0", "G4a", "bp1", "q4_0", "f0", "T7_1", "be1", "p4_0", "si3", "bp2", "p2_1", "be2", "G4b", "bp3",
-    "q3_1", "q3_0", "be3", "f2", "p3_0", "T8_0", "f1", "q5_0", "p3_1", "q5_1", "T8_1", "p5_0", "qs1",
-    "q4_1", "bp4", "f3", "be4", "p4_1", "q6_0", "T9_1", "bp5", "p6_0", "be5", "bp6", "p5_1", "be6",
-    "q7_0", "q6_1", "bp7", "p7_0", "be7", "f4", "T9_0", "p6_1", "q7_1", "f5", "p7_1", "f6", "f7",
+    "wd0", "wd1", "tx0", "tx1", "ex0", "tx2", "F0", "ex1", "tx3", "ex2", "F1", "tx4", "T1_0", "F2",
+    "wd2", "q0_2", "ex3", "ex4", "T2_0", "tw0_0", "T1_1", "F3", "t3a", "tw1_0", "tw0_1", "F4", "ew0_0",
+    "q0_3", "ew1_0", "t3b", "ew0_1", "G2b", "tw2_0", "tw1_1", "T2_1", "tw2_1", "wd3", "ew1_1", "ew2_0",
+    "T3_1", "tw3_0", "q1_2", "ew2_1", "tw3_1", "q1_1", "G2a", "q0_1", "tw4_0", "wd4", "qw1", "qw0",
+    "qw2", "T3_0", "ew3_1", "ew3_0", "ew4_0", "tw4_1", "q2_3", "Ha", "tw5_0", "q2_4", "T4_0", "tw5_1",
+    "q1_0", "xn", "q2_2", "q0_4", "ew5_1", "q2_1", "qw3", "ew5_0", "q0_0", "ew4_1", "p1_1", "T4_1", "Hb",
+    "tw7_0", "p1_0", "q2_0", "tw6_0", "qw4", "tw6_1", "qw5", "ew6_0", "p2_1", "q1_3", "ew6_1", "ew7_0",
+    "G3b", "T5_0", "tw8_1", "p0_0", "p0_1", "tw7_1", "tw8_0", "ew7_1", "ew8_0", "tw9_0", "ew8_1",
+    "tw9_1", "qw6", "p2_2", "m7b", "ew9_0", "p0_2", "ew9_1", "tn0", "p2_0", "G3a", "tn1", "qw7", "qw8",
+    "p0_3", "qw9", "si0", "q1_4", "p0_4", "m7a", "p1_2", "si1", "p1_4", "p1_3", "T6_0", "q3_0", "qs0",
+    "q3_2", "bp0", "T6_1", "p2_4", "tn2", "be0", "q4_0", "q3_1", "p3_0", "G4a", "q3_3", "bp1", "T7_1",
+    "p3_1", "p2_3", "p3_2", "be1", "si2", "bp2", "p3_3", "tn3", "f1", "T8_0", "f0", "G4b", "q5_0",
+    "q4_2", "p5_0", "q3_4", "q4_3", "p4_2", "q5_3", "q5_2", "p5_3", "T7_0", "be2", "p4_3", "si3", "q5_4",
+    "p5_2", "q4_1", "p5_4", "q5_1", "T8_2", "T9_3", "bp3", "p3_4", "be3", "q4_4", "p4_1", "qs1", "T8_3",
+    "p4_4", "f2", "bp4", "q6_1", "be4", "q6_3", "p6_1", "T9_0", "T8_1", "p5_1", "T9_1", "bp5", "p4_0",
+    "be5", "q6_4", "T8_4", "f3", "p6_4", "q7_1", "bp6", "q7_4", "p7_1", "be6", "f4", "p7_4", "T9_4",
+    "p6_3", "bp7", "q7_2", "q6_0", "be7", "p7_2", "q7_3", "T9_2", "p6_0", "p7_3", "q7_0", "q6_2", "p7_0",
+    "f5", "p6_2", "f7", "f6",
 )
 
 ON_VECTOR = (
-    "ex1", "ex2", "ex3", "T2_0", "T2_1", "T3_0", "T3_1", "T4_1", "T6_1", "T8_1", "ew0_0", "ew0_1",
-    "ew3_1", "ew7_1",
+    "ex1", "ex2", "ex3", "ex4", "T2_1", "T3_0", "T3_1", "T4_0", "T4_1", "T6_1", "ew7_0",
 )
+
+
+FINE = (8, 9)
 
 
 def runs_of(n):
@@ -51,7 +58,7 @@ def runs_of(n):
     for rho in range(ORD):
         s = 4 * n + rho
         c, m0 = s % ORD, 102 * n + s // ORD
-        if out and out[-1][3] == m0:
+        if out and out[-1][3] == m0 and not (n in FINE and c % 2 == 0):
             out[-1][1] = rho + 1
         else:
             out.append([rho, rho + 1, c, m0])
@@ -71,27 +78,19 @@ def tile_kantlinear_kernel(tc, x, base_weight_words, base_weight_scales, cheby_w
         ident = keep.tile([P, P], F32, name="ident")
         make_identity(nc, ident[:])
         ft = keep.tile([P, ORD, FTW], BF16, name="ft", align_bytes=64)
+        nc.gpsimd.memset(ft[:, :, 0:CW], 1.0)
+
         xs = keep.tile([P, 5120], BF16, name="xs", tag="raw0")
-        nc.vector.memset(xs[96:128, 0:2560].bitcast(F32), 0.0)
-        nc.gpsimd.memset(xs[96:128, 2560:5120].bitcast(F32), 0.0)
-        nc.vector.memset(ft[:, 0:5, 0:CW], 1.0)
-        nc.gpsimd.memset(ft[:, 5:10, 0:CW], 1.0)
-
         xrows = x[0:960, :].rearrange("(b r) i -> b r i", r=ORD)
-
-        def load_classes(ra, rb):
-            for pa, pb in ((32, 96), (0, 32)):
-                nc.sync.dma_start(
-                    out=xs[pa:pb, ra * 512 : rb * 512].rearrange("p (r i) -> p r i", r=rb - ra),
-                    in_=xrows[pa:pb, ra:rb, :],
-                )
-
-        load_classes(0, 2)
-        nc.sync.dma_start(out=xs[96:100, :], in_=x[960:1000, :].rearrange("(b r) i -> b (r i)", r=ORD))
-        nc.sync.dma_start(out=xs[100:102, :], in_=x[1000:1020, :].rearrange("(b r) i -> b (r i)", r=ORD))
+        nc.sync.dma_start(out=xs[103:128, :], in_=x[0:250, :].rearrange("(b r) i -> b (r i)", r=ORD))
+        nc.sync.dma_start(out=xs[96:102, :], in_=x[960:1020, :].rearrange("(b r) i -> b (r i)", r=ORD))
         nc.sync.dma_start(out=xs[102:103, 0:2048], in_=x[1020:1024, :].rearrange("(o r) i -> o (r i)", o=1))
-        load_classes(2, 6)
-        load_classes(6, 10)
+        nc.sync.dma_start(out=xs[102:103, 2048:5120], in_=x[0:6, :].rearrange("(o r) i -> o (r i)", o=1))
+        for k in range(5):
+            nc.sync.dma_start(
+                out=xs[0:96, k * 1024 : (k + 1) * 1024].rearrange("p (r i) -> p r i", r=2),
+                in_=xrows[:, 2 * k : 2 * k + 2, :],
+            )
 
         w4 = keep.tile([P, 2 * OUT], U8, name="w4", align_bytes=64)
         w4s = keep.tile([P, OUT], U8, name="w4s", align_bytes=64)
@@ -260,7 +259,7 @@ def tile_kantlinear_kernel(tc, x, base_weight_words, base_weight_scales, cheby_w
                 live["fw%d" % m] = keep.tile([P, ORD, P], U32, name="fw%d" % m, tag="fw%d" % (m % 3), align_bytes=64)
                 live["fs%d" % m] = keep.tile([P, ORD, P], U8, name="fs%d" % m, tag="fs%d" % (m % 3), align_bytes=64)
             lo = (m % 4) * 512
-            for c in range(5 * h, 5 * h + 5):
+            for c in range(2 * h, 2 * h + 2):
                 nc.vector.quantize_mx(
                     out=live["fw%d" % m][:, c, :].bitcast(FP8X4),
                     scales=live["fs%d" % m][:, c, :],
@@ -268,17 +267,19 @@ def tile_kantlinear_kernel(tc, x, base_weight_words, base_weight_scales, cheby_w
                 )
 
         def pt_(m, h):
-            if h == 0:
+            if ("acc%d" % m) not in live:
                 live["acc%d" % m] = ps.tile([P, OUT], F32, name="acc%d" % m, tag="acc%d" % (m % 4))
-            for c in range(5 * h, 5 * h + 5):
+                live["np%d" % m] = 0
+            for c in range(2 * h, 2 * h + 2):
+                live["np%d" % m] = live["np%d" % m] + 1
                 nc.tensor.matmul_mx(
                     out=live["acc%d" % m][:],
                     lhsT=live["fw%d" % m][:, c, :].bitcast(FP8X4),
                     lhsT_scale=live["fs%d" % m][:, c, :],
                     rhs=w_words[:, c, :].bitcast(FP8X4),
                     rhs_scale=w_scales[:, c, :],
-                    start=(c == 0),
-                    stop=(c == ORD - 1),
+                    start=(live["np%d" % m] == 1),
+                    stop=(live["np%d" % m] == ORD),
                 )
 
         def fo(m):
@@ -317,7 +318,7 @@ def tile_kantlinear_kernel(tc, x, base_weight_words, base_weight_scales, cheby_w
             steps["bp%d" % m] = (bp, (m,))
             steps["be%d" % m] = (be, (m,))
             steps["f%d" % m] = (fo, (m,))
-            for h in range(2):
+            for h in range(5):
                 steps["q%d_%d" % (m, h)] = (qt, (m, h))
                 steps["p%d_%d" % (m, h)] = (pt_, (m, h))
 

@@ -70,27 +70,27 @@ def tile_kantlinear_kernel(tc, x, base_weight_words, base_weight_scales, cheby_w
     with ExitStack() as ctx:
         keep = ctx.enter_context(tc.tile_pool(name="keep", bufs=1))
         ps = ctx.enter_context(tc.psum_pool(name="ps", bufs=1))
-        ctx.enter_context(tc.manual_schedule())
 
-        warm = keep.tile([P, 2], F32, name="warm")
-        nc.vector.memset(warm[:, 0:1], 0.0)
-        nc.scalar.activation(out=warm[:, 1:2], in_=warm[:, 0:1], func=ACT.Silu)
-        ident = keep.tile([P, P], F32, name="ident")
-        make_identity(nc, ident[:])
-        ft = keep.tile([P, ORD, FTW], BF16, name="ft", align_bytes=64)
-        nc.gpsimd.memset(ft[:, :, 0:CW], 1.0)
+        with tc.manual_schedule():
+            warm = keep.tile([P, 2], F32, name="warm")
+            nc.vector.memset(warm[:, 0:1], 0.0)
+            nc.scalar.activation(out=warm[:, 1:2], in_=warm[:, 0:1], func=ACT.Silu)
+            ident = keep.tile([P, P], F32, name="ident")
+            make_identity(nc, ident[:])
+            ft = keep.tile([P, ORD, FTW], BF16, name="ft", align_bytes=64)
+            nc.gpsimd.memset(ft[:, :, 0:CW], 1.0)
 
-        xs = keep.tile([P, 5120], BF16, name="xs", tag="raw0")
-        xrows = x[0:960, :].rearrange("(b r) i -> b r i", r=ORD)
-        nc.sync.dma_start(out=xs[103:128, :], in_=x[0:250, :].rearrange("(b r) i -> b (r i)", r=ORD))
-        nc.sync.dma_start(out=xs[96:102, :], in_=x[960:1020, :].rearrange("(b r) i -> b (r i)", r=ORD))
-        nc.sync.dma_start(out=xs[102:103, 0:2048], in_=x[1020:1024, :].rearrange("(o r) i -> o (r i)", o=1))
-        nc.sync.dma_start(out=xs[102:103, 2048:5120], in_=x[0:6, :].rearrange("(o r) i -> o (r i)", o=1))
-        for k in range(5):
-            nc.sync.dma_start(
-                out=xs[0:96, k * 1024 : (k + 1) * 1024].rearrange("p (r i) -> p r i", r=2),
-                in_=xrows[:, 2 * k : 2 * k + 2, :],
-            )
+            xs = keep.tile([P, 5120], BF16, name="xs", tag="raw0")
+            xrows = x[0:960, :].rearrange("(b r) i -> b r i", r=ORD)
+            nc.sync.dma_start(out=xs[103:128, :], in_=x[0:250, :].rearrange("(b r) i -> b (r i)", r=ORD))
+            nc.sync.dma_start(out=xs[96:102, :], in_=x[960:1020, :].rearrange("(b r) i -> b (r i)", r=ORD))
+            nc.sync.dma_start(out=xs[102:103, 0:2048], in_=x[1020:1024, :].rearrange("(o r) i -> o (r i)", o=1))
+            nc.sync.dma_start(out=xs[102:103, 2048:5120], in_=x[0:6, :].rearrange("(o r) i -> o (r i)", o=1))
+            for k in range(5):
+                nc.sync.dma_start(
+                    out=xs[0:96, k * 1024 : (k + 1) * 1024].rearrange("p (r i) -> p r i", r=2),
+                    in_=xrows[:, 2 * k : 2 * k + 2, :],
+                )
 
         w4 = keep.tile([P, 2 * OUT], U8, name="w4", align_bytes=64)
         w4s = keep.tile([P, OUT], U8, name="w4s", align_bytes=64)

@@ -14,315 +14,313 @@ ALU = mybir.AluOpType
 ACT = mybir.ActivationFunctionType
 
 P = 128
-B = 1024
-IN = 512
-OUT = 512
-ORD = 10
-NB = 104
-CW = NB * 4
-FTW = 2048 + 32
+ROWS = 1024
+FEATURES = 512
+OUTS = 512
+ORDERS = 10
+ROW_TILES = ROWS // P
+PASSES = ORDERS + 3
+CLASS_ROWS = 104
+CLASS_COLS = 4 * CLASS_ROWS
+FT_ROWS = 512
+FT_COLS = 4 * FT_ROWS + 32
+HALVES = ((0, 5), (5, 10))
 
-FLOPS = 2 * B * OUT * (IN + IN * ORD)
-
-ORDER = (
-    "wd0", "wd1", "tx0", "tx1", "ex0", "tx2", "F0", "ex1", "tx3", "ex2", "F1", "tx4", "T1_0", "F2",
-    "wd2", "q0_2", "ex3", "ex4", "T2_0", "tw0_0", "T1_1", "F3", "t3a", "tw1_0", "tw0_1", "F4", "ew0_0",
-    "q0_3", "ew1_0", "t3b", "ew0_1", "G2b", "tw2_0", "tw1_1", "T2_1", "tw2_1", "wd3", "ew1_1", "ew2_0",
-    "T3_1", "tw3_0", "q1_2", "ew2_1", "tw3_1", "q1_1", "G2a", "q0_1", "tw4_0", "wd4", "qw1", "qw0",
-    "qw2", "T3_0", "ew3_1", "ew3_0", "ew4_0", "tw4_1", "q2_3", "Ha", "tw5_0", "q2_4", "T4_0", "tw5_1",
-    "q1_0", "xn", "q2_2", "q0_4", "ew5_1", "q2_1", "qw3", "ew5_0", "q0_0", "ew4_1", "p1_1", "T4_1", "Hb",
-    "tw7_0", "p1_0", "q2_0", "tw6_0", "qw4", "tw6_1", "qw5", "ew6_0", "p2_1", "q1_3", "ew6_1", "ew7_0",
-    "G3b", "T5_0", "tw8_1", "p0_0", "p0_1", "tw7_1", "tw8_0", "ew7_1", "ew8_0", "tw9_0", "ew8_1",
-    "tw9_1", "qw6", "p2_2", "m7b", "ew9_0", "p0_2", "ew9_1", "tn0", "p2_0", "G3a", "tn1", "qw7", "qw8",
-    "p0_3", "qw9", "si0", "q1_4", "p0_4", "m7a", "p1_2", "si1", "p1_4", "p1_3", "T6_0", "q3_0", "qs0",
-    "q3_2", "bp0", "T6_1", "p2_4", "tn2", "be0", "q4_0", "q3_1", "p3_0", "G4a", "q3_3", "bp1", "T7_1",
-    "p3_1", "p2_3", "p3_2", "be1", "si2", "bp2", "p3_3", "tn3", "f1", "T8_0", "f0", "G4b", "q5_0",
-    "q4_2", "p5_0", "q3_4", "q4_3", "p4_2", "q5_3", "q5_2", "p5_3", "T7_0", "be2", "p4_3", "si3", "q5_4",
-    "p5_2", "q4_1", "p5_4", "q5_1", "T8_2", "T9_3", "bp3", "p3_4", "be3", "q4_4", "p4_1", "qs1", "T8_3",
-    "p4_4", "f2", "bp4", "q6_1", "be4", "q6_3", "p6_1", "T9_0", "T8_1", "p5_1", "T9_1", "bp5", "p4_0",
-    "be5", "q6_4", "T8_4", "f3", "p6_4", "q7_1", "bp6", "q7_4", "p7_1", "be6", "f4", "p7_4", "T9_4",
-    "p6_3", "bp7", "q7_2", "q6_0", "be7", "p7_2", "q7_3", "T9_2", "p6_0", "p7_3", "q7_0", "q6_2", "p7_0",
-    "f5", "p6_2", "f7", "f6",
-)
-
-ON_VECTOR = (
-    "ex1", "ex2", "ex3", "ex4", "T2_1", "T3_0", "T3_1", "T4_0", "T4_1", "T6_1", "ew7_0",
-)
+FLOPS = 2 * ROWS * OUTS * (FEATURES + FEATURES * ORDERS)
 
 
-FINE = (8, 9)
-
-
-def runs_of(n):
-    out = []
-    for rho in range(ORD):
-        s = 4 * n + rho
-        c, m0 = s % ORD, 102 * n + s // ORD
-        if out and out[-1][3] == m0 and not (n in FINE and c % 2 == 0):
-            out[-1][1] = rho + 1
-        else:
-            out.append([rho, rho + 1, c, m0])
-    return out
+def class_runs(order):
+    wrap = (ORDERS - 4 * order % ORDERS) % ORDERS
+    return [(0, wrap), (wrap, ORDERS - wrap)] if wrap else [(0, ORDERS)]
 
 
 def tile_kantlinear_kernel(tc, x, base_weight_words, base_weight_scales, cheby_weight, out):
     nc = tc.nc
     with ExitStack() as ctx:
         keep = ctx.enter_context(tc.tile_pool(name="keep", bufs=1))
-        ps = ctx.enter_context(tc.psum_pool(name="ps", bufs=1))
+        loads = ctx.enter_context(tc.tile_pool(name="loads", bufs=3))
+        grouped = ctx.enter_context(tc.tile_pool(name="grouped", bufs=3))
+        flat_mx = ctx.enter_context(tc.tile_pool(name="flat_mx", bufs=4))
+        results = ctx.enter_context(tc.tile_pool(name="results", bufs=3))
+        turned = ctx.enter_context(tc.psum_pool(name="turned", bufs=3))
+        sums = ctx.enter_context(tc.psum_pool(name="sums", bufs=5))
+
+        w_rows = cheby_weight.rearrange("o i k -> o (i k)")
+
+        def load_w(pair):
+            tile = loads.tile([P, 5120], BF16, name="w_raw", tag="load")
+            nc.sync.dma_start(
+                out=tile[:, 0:4096].rearrange("p (t j) -> p t j", t=4),
+                in_=w_rows[:, pair * 1024 : (pair + 1) * 1024].rearrange("(t o) j -> o t j", o=P),
+            )
+            return tile
 
         with tc.manual_schedule():
             warm = keep.tile([P, 2], F32, name="warm")
             nc.vector.memset(warm[:, 0:1], 0.0)
             nc.scalar.activation(out=warm[:, 1:2], in_=warm[:, 0:1], func=ACT.Silu)
+
             ident = keep.tile([P, P], F32, name="ident")
             make_identity(nc, ident[:])
-            ft = keep.tile([P, ORD, FTW], BF16, name="ft", align_bytes=64)
-            nc.gpsimd.memset(ft[:, :, 0:CW], 1.0)
 
-            xs = keep.tile([P, 5120], BF16, name="xs", tag="raw0")
-            xrows = x[0:960, :].rearrange("(b r) i -> b r i", r=ORD)
-            nc.sync.dma_start(out=xs[103:128, :], in_=x[0:250, :].rearrange("(b r) i -> b (r i)", r=ORD))
-            nc.sync.dma_start(out=xs[96:102, :], in_=x[960:1020, :].rearrange("(b r) i -> b (r i)", r=ORD))
-            nc.sync.dma_start(out=xs[102:103, 0:2048], in_=x[1020:1024, :].rearrange("(o r) i -> o (r i)", o=1))
-            nc.sync.dma_start(out=xs[102:103, 2048:5120], in_=x[0:6, :].rearrange("(o r) i -> o (r i)", o=1))
+            ft = keep.tile([P, ORDERS, FT_COLS], BF16, name="ft", align_bytes=64)
+            nc.gpsimd.memset(ft[:, :, 0:CLASS_COLS], 1.0)
+
+            x_sorted = loads.tile([P, 5120], BF16, name="x_sorted", tag="load")
+            ten_rows = "(b r) i -> b (r i)"
+            nc.sync.dma_start(out=x_sorted[103:128, :], in_=x[0:250, :].rearrange(ten_rows, r=ORDERS))
+            nc.sync.dma_start(out=x_sorted[96:102, :], in_=x[960:1020, :].rearrange(ten_rows, r=ORDERS))
+            nc.sync.dma_start(out=x_sorted[102:103, 0:2048], in_=x[1020:1024, :].rearrange(ten_rows, r=4))
+            nc.sync.dma_start(out=x_sorted[102:103, 2048:5120], in_=x[0:6, :].rearrange(ten_rows, r=6))
+            by_class = x[0:960, :].rearrange("(b r) i -> b r i", r=ORDERS)
             for k in range(5):
                 nc.sync.dma_start(
-                    out=xs[0:96, k * 1024 : (k + 1) * 1024].rearrange("p (r i) -> p r i", r=2),
-                    in_=xrows[:, 2 * k : 2 * k + 2, :],
+                    out=x_sorted[0:96, k * 1024 : (k + 1) * 1024].rearrange("p (r i) -> p r i", r=2),
+                    in_=by_class[:, 2 * k : 2 * k + 2, :],
+                )
+            w_raw = {0: load_w(0), 1: load_w(1)}
+
+        w4_words = keep.tile([P, 2 * OUTS], U8, name="w4_words", align_bytes=64)
+        w4_scales = keep.tile([P, OUTS], U8, name="w4_scales", align_bytes=64)
+        nc.vector.memset(w4_scales[:].bitcast(I32), 0)
+
+        xt = keep.tile([P, ORDERS, CLASS_COLS], BF16, name="xt")
+        sq_a = keep.tile([P, ORDERS, CLASS_COLS], F32, name="sq_a")
+        sq_b = keep.tile([P, ORDERS, CLASS_COLS], F32, name="sq_b")
+        sq_c = keep.tile([P, ORDERS, CLASS_COLS], F32, name="sq_c")
+        t3 = keep.tile([P, ORDERS, CLASS_COLS], F32, name="t3")
+
+        w_words = keep.tile([P, ORDERS, OUTS], U32, name="w_words", align_bytes=64)
+        w_scales = keep.tile([P, ORDERS, OUTS], U8, name="w_scales", align_bytes=64)
+        silu_words = keep.tile([P, 2, ROWS], U32, name="silu_words", align_bytes=64)
+        silu_scales = keep.tile([P, 2, ROWS], U8, name="silu_scales", align_bytes=64)
+
+        def square(dst, src, scale, bias):
+            for a, b in HALVES:
+                nc.scalar.activation(out=dst[:, a:b, :], in_=src[:, a:b, :], func=ACT.Square, bias=bias, scale=scale)
+
+        def shifted_product(dst, in0, shift, in1):
+            nc.vector.scalar_tensor_tensor(out=dst, in0=in0, scalar=shift, in1=in1, op0=ALU.add, op1=ALU.mult)
+
+        def place(order, first, count):
+            s = 4 * order + first
+            chunk, row = s % ORDERS, (102 * order + s // ORDERS) % FT_ROWS
+            return ft[:, chunk : chunk + count, 4 * row : 4 * row + CLASS_COLS]
+
+        def half_minus_one(engine, order, src, first, count):
+            if engine == "vector":
+                nc.vector.tensor_scalar(
+                    out=place(order, first, count),
+                    in0=src[:, first : first + count, :],
+                    scalar1=0.5,
+                    scalar2=-1.0,
+                    op0=ALU.mult,
+                    op1=ALU.add,
+                )
+            else:
+                nc.scalar.activation(
+                    out=place(order, first, count), in_=src[:, first : first + count, :], func=ACT.Copy, bias=-1.0, scale=0.5
                 )
 
-        w4 = keep.tile([P, 2 * OUT], U8, name="w4", align_bytes=64)
-        w4s = keep.tile([P, OUT], U8, name="w4s", align_bytes=64)
-        nc.vector.memset(w4s[:].bitcast(I32), 0)
+        def prepare_w(pair):
+            words = w_raw[pair][:].bitcast(F32)
+            for chunk in (2 * pair, 2 * pair + 1):
+                w_grouped = grouped.tile([P, 4 * OUTS], BF16, name="w_grouped", tag="grouped", align_bytes=64)
+                pairs_out = w_grouped[:].bitcast(F32).rearrange("p (o u) -> p o u", u=2)
+                for half in range(2):
+                    bank = turned.tile([P, 2, 2 * P], F32, name="w_turned", tag="turned")
+                    for block in range(2):
+                        for u in range(2):
+                            lo = (2 * half + block) * 512 + (chunk % 2) * 256 + u * P
+                            nc.tensor.transpose(bank[:, u, block * P : (block + 1) * P], words[:, lo : lo + P], ident[:])
+                    nc.scalar.copy(
+                        out=pairs_out[:, half * 256 : (half + 1) * 256, :], in_=bank[:].rearrange("p u o -> p o u"))
+                nc.vector.quantize_mx(
+                    out=w_words[:, chunk, :].bitcast(FP8X4), scales=w_scales[:, chunk, :], in_=w_grouped[:])
 
-        cw = cheby_weight.rearrange("o i k -> o (i k)")
+        mx = {}
+        acc = {}
+        passes = {}
 
-        xt = keep.tile([P, ORD, CW], BF16, name="xt")
-        ta = keep.tile([P, ORD, CW], F32, name="ta")
-        tb = keep.tile([P, ORD, CW], F32, name="tb")
-        te = keep.tile([P, ORD, CW], F32, name="te")
-        t3 = keep.tile([P, ORD, CW], F32, name="t3")
+        def quantise_rows(tile, chunks):
+            if tile not in mx:
+                mx[tile] = (
+                    flat_mx.tile([P, ORDERS, P], U32, name="flat_words", align_bytes=64),
+                    flat_mx.tile([P, ORDERS, P], U8, name="flat_scales", align_bytes=64),
+                )
+            lo = (tile % 4) * 4 * P
+            for c in chunks:
+                nc.vector.quantize_mx(
+                    out=mx[tile][0][:, c, :].bitcast(FP8X4), scales=mx[tile][1][:, c, :], in_=ft[:, c, lo : lo + 4 * P])
 
-        w_words = keep.tile([P, ORD, OUT], U32, name="w_words", align_bytes=64)
-        w_scales = keep.tile([P, ORD, OUT], U8, name="w_scales", align_bytes=64)
-        s_words = keep.tile([P, B], U32, name="s_words", align_bytes=64)
-        s_scales = keep.tile([P, B], U8, name="s_scales", align_bytes=64)
-        base_sb = keep.tile([P, 8, OUT], F32, name="base_sb")
+        def one_pass(tile, lhsT, lhsT_scale, rhs, rhs_scale):
+            if tile not in acc:
+                acc[tile] = sums.tile([P, OUTS], F32, name="acc")
+                passes[tile] = 0
+            passes[tile] = passes[tile] + 1
+            nc.tensor.matmul_mx(
+                out=acc[tile][:],
+                lhsT=lhsT,
+                lhsT_scale=lhsT_scale,
+                rhs=rhs,
+                rhs_scale=rhs_scale,
+                start=(passes[tile] == 1),
+                stop=(passes[tile] == PASSES),
+            )
 
-        xs_w = xs[:].bitcast(F32)
-        xt_w = xt[:].bitcast(F32)
-        live = {}
-        steps = {}
+        def multiply_rows(tile, chunks):
+            for c in chunks:
+                one_pass(
+                    tile,
+                    mx[tile][0][:, c, :].bitcast(FP8X4),
+                    mx[tile][1][:, c, :],
+                    w_words[:, c, :].bitcast(FP8X4),
+                    w_scales[:, c, :],
+                )
 
-        def tp_tile(idx, shape):
-            return ps.tile(shape, F32, name="tp_%d" % idx, tag="tp%d" % (idx % 3))
+        def add_base(tile):
+            rows = slice(tile * P, (tile + 1) * P)
+            for which in (0, 0, 1):
+                one_pass(
+                    tile,
+                    silu_words[:, which, rows].bitcast(FP8X4),
+                    silu_scales[:, which, rows],
+                    w4_words[:].bitcast(FP4X4),
+                    w4_scales[:],
+                )
 
-        def copy_on(name, dst, src):
-            if name in ON_VECTOR:
-                nc.vector.tensor_copy(out=dst, in_=src)
+        def finish_rows(tile, engine):
+            res = results.tile([P, OUTS], F32, name="res")
+            if engine == "vector":
+                nc.vector.tensor_scalar(out=res[:], in0=acc[tile][:], scalar1=0.1, scalar2=None, op0=ALU.mult)
             else:
-                nc.scalar.copy(out=dst, in_=src)
+                nc.scalar.mul(out=res[:], in_=acc[tile][:], mul=0.1)
+            nc.sync.dma_start(out=out[tile * P : (tile + 1) * P, :], in_=res[:])
 
-        def tx(k):
-            pt = tp_tile(k, [P, 2, 2, P])
-            live["pt%d" % k] = pt
+        def quantise_silu(x_natural, half):
+            words = x_natural[:].bitcast(F32)
+            silu = grouped.tile([P, 2048], BF16, name="silu", tag="grouped", align_bytes=64)
+            for k in range(2):
+                bank = turned.tile([P, 2, 2 * P], F32, name="x_turned", tag="turned")
+                for block in range(2):
+                    j = 4 * half + 2 * k + block
+                    for u in range(2):
+                        nc.tensor.transpose(
+                            bank[:, u, block * P : (block + 1) * P], words[:, j * 256 + u : (j + 1) * 256 : 2], ident[:])
+                nc.scalar.activation(
+                    out=silu[:, k * 1024 : (k + 1) * 1024].rearrange("p (q u e) -> p q u e", u=2, e=2),
+                    in_=bank[:].bitcast(BF16).rearrange("p u (q e) -> p q u e", e=2),
+                    func=ACT.Silu,
+                )
+            cols = slice(half * 512, (half + 1) * 512)
+            nc.vector.quantize_mx(out=silu_words[:, 0, cols].bitcast(FP8X4), scales=silu_scales[:, 0, cols], in_=silu[:])
+            nc.vector.tensor_scalar(out=silu[:], in0=silu[:], scalar1=8.0, scalar2=None, op0=ALU.mult)
+            nc.vector.quantize_mx(out=silu_words[:, 1, cols].bitcast(FP8X4), scales=silu_scales[:, 1, cols], in_=silu[:])
+
+        all_chunks = range(ORDERS)
+
+        sorted_words = x_sorted[:].bitcast(F32)
+        xt_words = xt[:].bitcast(F32)
+        for k in range(5):
+            bank = turned.tile([P, 2, 2, P], F32, name="xs_turned", tag="turned")
             for r in range(2):
                 for u in range(2):
                     lo = (2 * k + r) * 256 + u * P
-                    nc.tensor.transpose(pt[:, r, u, :], xs_w[:, lo : lo + P], ident[:])
-
-        def ex(k):
-            copy_on(
-                "ex%d" % k,
-                xt_w[:, 2 * k : 2 * k + 2, :].rearrange("p r (b u) -> p r b u", u=2),
-                live["pt%d" % k][:, :, :, 0:NB].rearrange("p r u b -> p r b u"),
+                    nc.tensor.transpose(bank[:, r, u, :], sorted_words[:, lo : lo + P], ident[:])
+            nc.vector.tensor_copy(
+                out=xt_words[:, 2 * k : 2 * k + 2, :].rearrange("p r (b u) -> p r b u", u=2),
+                in_=bank[:, :, :, 0:CLASS_ROWS].rearrange("p r u b -> p r b u"),
             )
-
-        def sq(dst, src, a, b, scale, bias):
-            nc.scalar.activation(out=dst[:, a:b, :], in_=src[:, a:b, :], func=ACT.Square, bias=bias, scale=scale)
-
-        def stt(dst, in0, scalar, in1):
-            nc.vector.scalar_tensor_tensor(out=dst, in0=in0, scalar=scalar, in1=in1, op0=ALU.add, op1=ALU.mult)
-
-        def fin(n, j):
-            ra, rb, ca, m0 = runs_of(n)[j]
-            mm = m0 % 512
-            dst = ft[:, ca : ca + (rb - ra), 4 * mm : 4 * mm + CW]
-            if n == 1:
-                nc.vector.tensor_copy(out=dst, in_=xt[:, ra:rb, :])
-            elif n in (2, 4, 6, 8):
-                src = {2: ta, 4: tb, 6: ta, 8: tb}[n]
-                if ("T%d_%d" % (n, j)) in ON_VECTOR:
-                    nc.vector.tensor_scalar(
-                        out=dst, in0=src[:, ra:rb, :], scalar1=0.5, scalar2=-1.0, op0=ALU.mult, op1=ALU.add)
-                else:
-                    nc.scalar.activation(out=dst, in_=src[:, ra:rb, :], func=ACT.Copy, bias=-1.0, scale=0.5)
-            elif n == 3:
-                copy_on("T3_%d" % j, dst, t3[:, ra:rb, :])
-            elif n == 5:
-                stt(dst, te[:, ra:rb, :], -1.25, xt[:, ra:rb, :])
-            elif n == 7:
-                nc.vector.tensor_tensor(out=dst, in0=te[:, ra:rb, :], in1=xt[:, ra:rb, :], op=ALU.subtract)
-            else:
-                stt(dst, ta[:, ra:rb, :], -3.0, t3[:, ra:rb, :])
-
-        def wd(g):
-            wr = keep.tile([P, 5120], BF16, name="wr%d" % g, tag="raw%d" % ((g + 1) % 3))
-            live["wr%d" % g] = wr
-            nc.sync.dma_start(
-                out=wr[:, 0:4096].rearrange("p (t j) -> p t j", t=4),
-                in_=cw[:, g * 1024 : (g + 1) * 1024].rearrange("(t o) j -> o t j", o=P),
-            )
-
-        def tw(c, h):
-            pw = tp_tile(5 + 2 * c + h, [P, 2, 2 * P])
-            live["pw%d_%d" % (c, h)] = pw
-            wr_w = live["wr%d" % (c // 2)][:].bitcast(F32)
-            for ol in range(2):
-                for u in range(2):
-                    lo = (2 * h + ol) * 512 + (c % 2) * 256 + u * P
-                    nc.tensor.transpose(pw[:, u, ol * P : (ol + 1) * P], wr_w[:, lo : lo + P], ident[:])
-
-        def ew(c, h):
-            key = "wtg%d" % c
-            if key not in live:
-                live[key] = keep.tile([P, 2048], BF16, name=key, tag="grp%d" % (c % 3), align_bytes=64)
-            wtg_w = live[key][:].bitcast(F32).rearrange("p (o u) -> p o u", u=2)
-            copy_on(
-                "ew%d_%d" % (c, h),
-                wtg_w[:, h * 256 : (h + 1) * 256, :],
-                live["pw%d_%d" % (c, h)][:].rearrange("p u o -> p o u"),
-            )
-
-        def qw(c):
-            nc.vector.quantize_mx(
-                out=w_words[:, c, :].bitcast(FP8X4), scales=w_scales[:, c, :], in_=live["wtg%d" % c][:])
-
-        def xn_load():
-            xn = keep.tile([P, 5120], BF16, name="xn", tag="raw0")
-            live["xn"] = xn
-            nc.sync.dma_start(
-                out=xn[:, 0:4096].rearrange("p (j i) -> p j i", j=8), in_=x.rearrange("(j q) i -> q j i", q=P))
-            nc.sync.dma_start(out=w4[:].bitcast(I32), in_=base_weight_words[0].bitcast(I32))
-            for q in range(4):
-                nc.sync.dma_start(
-                    out=w4s[32 * q : 32 * q + 4, :].bitcast(I32),
-                    in_=base_weight_scales[0, 4 * q : 4 * q + 4, :].bitcast(I32),
-                )
-
-        def tn(k):
-            pn = tp_tile(25 + k, [P, 2, 2 * P])
-            live["pn%d" % k] = pn
-            xn_w = live["xn"][:].bitcast(F32)
-            for jj in range(2):
-                j = 2 * k + jj
-                for u in range(2):
-                    nc.tensor.transpose(
-                        pn[:, u, jj * P : (jj + 1) * P], xn_w[:, j * 256 + u : (j + 1) * 256 : 2], ident[:])
-
-        def si(k):
-            key = "sil%d" % (k // 2)
-            if key not in live:
-                live[key] = keep.tile([P, 2048], BF16, name=key, tag="grp%d" % (1 + k // 2), align_bytes=64)
             nc.scalar.activation(
-                out=live[key][:, (k % 2) * 1024 : (k % 2 + 1) * 1024].rearrange("p (q u e) -> p q u e", u=2, e=2),
-                in_=live["pn%d" % k][:].bitcast(BF16).rearrange("p u (q e) -> p q u e", e=2),
-                func=ACT.Silu,
+                out=sq_a[:, 2 * k : 2 * k + 2, :], in_=xt[:, 2 * k : 2 * k + 2, :], func=ACT.Square, scale=2.0)
+
+        for first, count in class_runs(1):
+            nc.vector.tensor_copy(out=place(1, first, count), in_=xt[:, first : first + count, :])
+        quantise_rows(0, all_chunks)
+        prepare_w(0)
+
+        for a, b in HALVES:
+            shifted_product(t3[:, a:b, :], sq_a[:, a:b, :], -3.0, xt[:, a:b, :])
+        for first, count in class_runs(2):
+            half_minus_one("vector", 2, sq_a, first, count)
+        quantise_rows(1, all_chunks)
+        prepare_w(1)
+
+        square(sq_b, sq_a, 1.0, -2.0)
+        for first, count in class_runs(3):
+            nc.vector.tensor_copy(out=place(3, first, count), in_=t3[:, first : first + count, :])
+        quantise_rows(2, all_chunks)
+        w_raw[2] = load_w(2)
+        prepare_w(2)
+
+        square(sq_c, sq_a, 1.0, -2.5)
+        for first, count in class_runs(4):
+            half_minus_one("vector", 4, sq_b, first, count)
+        quantise_rows(3, all_chunks)
+        w_raw[3] = load_w(3)
+        prepare_w(3)
+
+        for first, count in class_runs(5):
+            shifted_product(place(5, first, count), sq_c[:, first : first + count, :], -1.25, xt[:, first : first + count, :])
+        w_raw[4] = load_w(4)
+        prepare_w(4)
+
+        multiply_rows(0, all_chunks)
+        multiply_rows(1, all_chunks)
+        square(sq_a, t3, 2.0, 0.0)
+        for a, b in HALVES:
+            shifted_product(sq_c[:, a:b, :], sq_b[:, a:b, :], -2.0, t3[:, a:b, :])
+        multiply_rows(2, all_chunks)
+        multiply_rows(3, all_chunks)
+
+        x_natural = loads.tile([P, 5120], BF16, name="x_natural", tag="load")
+        nc.sync.dma_start(
+            out=x_natural[:, 0:4096].rearrange("p (j i) -> p j i", j=ROW_TILES), in_=x.rearrange("(j q) i -> q j i", q=P))
+        nc.sync.dma_start(out=w4_words[:].bitcast(I32), in_=base_weight_words[0].bitcast(I32))
+        for quadrant in range(4):
+            nc.sync.dma_start(
+                out=w4_scales[32 * quadrant : 32 * quadrant + 4, :].bitcast(I32),
+                in_=base_weight_scales[0, 4 * quadrant : 4 * quadrant + 4, :].bitcast(I32),
             )
+        quantise_silu(x_natural, 0)
+        for tile in range(4):
+            add_base(tile)
+            finish_rows(tile, "scalar")
 
-        def qs(h):
-            nc.vector.quantize_mx(
-                out=s_words[:, h * 512 : (h + 1) * 512].bitcast(FP8X4),
-                scales=s_scales[:, h * 512 : (h + 1) * 512],
-                in_=live["sil%d" % h][:],
+        (first_a, count_a), (first_b, count_b) = class_runs(6)
+        half_minus_one("scalar", 6, sq_a, first_a, count_a)
+        half_minus_one("vector", 6, sq_a, first_b, count_b)
+        for pair in range(5):
+            quantise_rows(4, (2 * pair, 2 * pair + 1))
+            multiply_rows(4, (2 * pair, 2 * pair + 1))
+
+        for first, count in class_runs(7):
+            nc.vector.tensor_tensor(
+                out=place(7, first, count),
+                in0=sq_c[:, first : first + count, :],
+                in1=xt[:, first : first + count, :],
+                op=ALU.subtract,
             )
+        square(sq_b, sq_b, 1.0, -2.0)
+        for pair in range(5):
+            quantise_rows(5, (2 * pair, 2 * pair + 1))
+            multiply_rows(5, (2 * pair, 2 * pair + 1))
 
-        def bp(m):
-            pb = ps.tile([P, OUT], F32, name="pb%d" % m, tag="bb")
-            live["pb%d" % m] = pb
-            nc.tensor.matmul_mx(
-                out=pb[:],
-                lhsT=s_words[:, m * P : (m + 1) * P].bitcast(FP8X4),
-                lhsT_scale=s_scales[:, m * P : (m + 1) * P],
-                rhs=w4[:].bitcast(FP4X4),
-                rhs_scale=w4s[:],
-                start=True,
-                stop=True,
-            )
+        quantise_silu(x_natural, 1)
+        for tile in (4, 5):
+            add_base(tile)
+            finish_rows(tile, "scalar")
+        add_base(6)
+        add_base(7)
 
-        def be(m):
-            copy_on("be%d" % m, base_sb[:, m, :], live["pb%d" % m][:])
-
-        def qt(m, h):
-            if ("fw%d" % m) not in live:
-                live["fw%d" % m] = keep.tile([P, ORD, P], U32, name="fw%d" % m, tag="fw%d" % (m % 3), align_bytes=64)
-                live["fs%d" % m] = keep.tile([P, ORD, P], U8, name="fs%d" % m, tag="fs%d" % (m % 3), align_bytes=64)
-            lo = (m % 4) * 512
-            for c in range(2 * h, 2 * h + 2):
-                nc.vector.quantize_mx(
-                    out=live["fw%d" % m][:, c, :].bitcast(FP8X4),
-                    scales=live["fs%d" % m][:, c, :],
-                    in_=ft[:, c, lo : lo + 512],
-                )
-
-        def pt_(m, h):
-            if ("acc%d" % m) not in live:
-                live["acc%d" % m] = ps.tile([P, OUT], F32, name="acc%d" % m, tag="acc%d" % (m % 4))
-                live["np%d" % m] = 0
-            for c in range(2 * h, 2 * h + 2):
-                live["np%d" % m] = live["np%d" % m] + 1
-                nc.tensor.matmul_mx(
-                    out=live["acc%d" % m][:],
-                    lhsT=live["fw%d" % m][:, c, :].bitcast(FP8X4),
-                    lhsT_scale=live["fs%d" % m][:, c, :],
-                    rhs=w_words[:, c, :].bitcast(FP8X4),
-                    rhs_scale=w_scales[:, c, :],
-                    start=(live["np%d" % m] == 1),
-                    stop=(live["np%d" % m] == ORD),
-                )
-
-        def fo(m):
-            res = keep.tile([P, OUT], F32, name="res%d" % m, tag="res%d" % (m % 3))
-            nc.vector.scalar_tensor_tensor(
-                out=res[:], in0=live["acc%d" % m][:], scalar=0.1, in1=base_sb[:, m, :], op0=ALU.mult, op1=ALU.add)
-            nc.sync.dma_start(out=out[m * P : (m + 1) * P, :], in_=res[:])
-
-        for k in range(5):
-            steps["tx%d" % k] = (tx, (k,))
-            steps["ex%d" % k] = (ex, (k,))
-            steps["F%d" % k] = (sq, (ta, xt, 2 * k, 2 * k + 2, 2.0, 0.0))
-            steps["wd%d" % k] = (wd, (k,))
-        for n in range(1, ORD):
-            for j in range(len(runs_of(n))):
-                steps["T%d_%d" % (n, j)] = (fin, (n, j))
-        for hn, a, b in (("a", 0, 5), ("b", 5, 10)):
-            steps["t3" + hn] = (stt, (t3[:, a:b, :], ta[:, a:b, :], -3.0, xt[:, a:b, :]))
-            steps["G2" + hn] = (sq, (tb, ta, a, b, 1.0, -2.0))
-            steps["H" + hn] = (sq, (te, ta, a, b, 1.0, -2.5))
-            steps["G3" + hn] = (sq, (ta, t3, a, b, 2.0, 0.0))
-            steps["m7" + hn] = (stt, (te[:, a:b, :], tb[:, a:b, :], -2.0, t3[:, a:b, :]))
-            steps["G4" + hn] = (sq, (tb, tb, a, b, 1.0, -2.0))
-        for c in range(ORD):
-            steps["qw%d" % c] = (qw, (c,))
-            for h in range(2):
-                steps["tw%d_%d" % (c, h)] = (tw, (c, h))
-                steps["ew%d_%d" % (c, h)] = (ew, (c, h))
-        steps["xn"] = (xn_load, ())
-        for k in range(4):
-            steps["tn%d" % k] = (tn, (k,))
-            steps["si%d" % k] = (si, (k,))
-        for h in range(2):
-            steps["qs%d" % h] = (qs, (h,))
-        for m in range(8):
-            steps["bp%d" % m] = (bp, (m,))
-            steps["be%d" % m] = (be, (m,))
-            steps["f%d" % m] = (fo, (m,))
-            for h in range(5):
-                steps["q%d_%d" % (m, h)] = (qt, (m, h))
-                steps["p%d_%d" % (m, h)] = (pt_, (m, h))
-
-        assert len(ORDER) == len(steps)
-        for name in ORDER:
-            fn, args = steps[name]
-            fn(*args)
+        for pair in range(5):
+            chunks = (2 * pair, 2 * pair + 1)
+            first = (2 * pair - 4 * 8) % ORDERS
+            half_minus_one("scalar", 8, sq_b, first, 2)
+            first = (2 * pair - 4 * 9) % ORDERS
+            shifted_product(place(9, first, 2), sq_a[:, first : first + 2, :], -3.0, t3[:, first : first + 2, :])
+            for tile in (6, 7):
+                quantise_rows(tile, chunks)
+                multiply_rows(tile, chunks)
+        finish_rows(6, "scalar")
+        finish_rows(7, "vector")

@@ -34,6 +34,10 @@ def class_runs(order):
     return [(0, wrap), (wrap, ORDERS - wrap)] if wrap else [(0, ORDERS)]
 
 
+def chunk_order(order):
+    return [(4 * order + rho) % ORDERS for rho in range(ORDERS)]
+
+
 def tile_kantlinear_kernel(tc, x, base_weight_words, base_weight_scales, cheby_weight, out):
     nc = tc.nc
     with ExitStack() as ctx:
@@ -212,12 +216,18 @@ def tile_kantlinear_kernel(tc, x, base_weight_words, base_weight_scales, cheby_w
                     in_=bank[:].bitcast(BF16).rearrange("p u (q e) -> p q u e", e=2),
                     func=ACT.Silu,
                 )
-            cols = slice(half * 512, (half + 1) * 512)
-            nc.vector.quantize_mx(out=silu_words[:, 0, cols].bitcast(FP8X4), scales=silu_scales[:, 0, cols], in_=silu[:])
-            nc.vector.tensor_scalar(out=silu[:], in0=silu[:], scalar1=8.0, scalar2=None, op0=ALU.mult)
-            nc.vector.quantize_mx(out=silu_words[:, 1, cols].bitcast(FP8X4), scales=silu_scales[:, 1, cols], in_=silu[:])
-
-        all_chunks = range(ORDERS)
+            for which in range(2):
+                for k in range(2):
+                    rows = slice(half * 512 + k * 256, half * 512 + (k + 1) * 256)
+                    nc.vector.quantize_mx(
+                        out=silu_words[:, which, rows].bitcast(FP8X4),
+                        scales=silu_scales[:, which, rows],
+                        in_=silu[:, k * 1024 : (k + 1) * 1024],
+                    )
+                if which == 0:
+                    for k in range(2):
+                        part = silu[:, k * 1024 : (k + 1) * 1024]
+                        nc.vector.tensor_scalar(out=part, in0=part, scalar1=8.0, scalar2=None, op0=ALU.mult)
 
         sorted_words = x_sorted[:].bitcast(F32)
         xt_words = xt[:].bitcast(F32)
@@ -236,27 +246,27 @@ def tile_kantlinear_kernel(tc, x, base_weight_words, base_weight_scales, cheby_w
 
         for first, count in class_runs(1):
             nc.vector.tensor_copy(out=place(1, first, count), in_=xt[:, first : first + count, :])
-        quantise_rows(0, all_chunks)
+        quantise_rows(0, chunk_order(1))
         prepare_w(0)
 
         for a, b in HALVES:
             shifted_product(t3[:, a:b, :], sq_a[:, a:b, :], -3.0, xt[:, a:b, :])
         for first, count in class_runs(2):
             half_minus_one("vector", 2, sq_a, first, count)
-        quantise_rows(1, all_chunks)
+        quantise_rows(1, chunk_order(2))
         prepare_w(1)
 
         square(sq_b, sq_a, 1.0, -2.0)
         for first, count in class_runs(3):
             nc.vector.tensor_copy(out=place(3, first, count), in_=t3[:, first : first + count, :])
-        quantise_rows(2, all_chunks)
+        quantise_rows(2, chunk_order(3))
         w_raw[2] = load_w(2)
         prepare_w(2)
 
         square(sq_c, sq_a, 1.0, -2.5)
         for first, count in class_runs(4):
             half_minus_one("vector", 4, sq_b, first, count)
-        quantise_rows(3, all_chunks)
+        quantise_rows(3, chunk_order(4))
         w_raw[3] = load_w(3)
         prepare_w(3)
 
@@ -265,13 +275,13 @@ def tile_kantlinear_kernel(tc, x, base_weight_words, base_weight_scales, cheby_w
         w_raw[4] = load_w(4)
         prepare_w(4)
 
-        multiply_rows(0, all_chunks)
-        multiply_rows(1, all_chunks)
+        multiply_rows(0, chunk_order(1))
+        multiply_rows(1, chunk_order(2))
         square(sq_a, t3, 2.0, 0.0)
         for a, b in HALVES:
             shifted_product(sq_c[:, a:b, :], sq_b[:, a:b, :], -2.0, t3[:, a:b, :])
-        multiply_rows(2, all_chunks)
-        multiply_rows(3, all_chunks)
+        multiply_rows(2, chunk_order(3))
+        multiply_rows(3, chunk_order(4))
 
         x_natural = loads.tile([P, 5120], BF16, name="x_natural", tag="load")
         nc.sync.dma_start(
@@ -291,8 +301,8 @@ def tile_kantlinear_kernel(tc, x, base_weight_words, base_weight_scales, cheby_w
         half_minus_one("scalar", 6, sq_a, first_a, count_a)
         half_minus_one("vector", 6, sq_a, first_b, count_b)
         for pair in range(5):
-            quantise_rows(4, (2 * pair, 2 * pair + 1))
-            multiply_rows(4, (2 * pair, 2 * pair + 1))
+            quantise_rows(4, chunk_order(6)[2 * pair : 2 * pair + 2])
+            multiply_rows(4, chunk_order(6)[2 * pair : 2 * pair + 2])
 
         for first, count in class_runs(7):
             nc.vector.tensor_tensor(
@@ -303,8 +313,8 @@ def tile_kantlinear_kernel(tc, x, base_weight_words, base_weight_scales, cheby_w
             )
         square(sq_b, sq_b, 1.0, -2.0)
         for pair in range(5):
-            quantise_rows(5, (2 * pair, 2 * pair + 1))
-            multiply_rows(5, (2 * pair, 2 * pair + 1))
+            quantise_rows(5, chunk_order(7)[2 * pair : 2 * pair + 2])
+            multiply_rows(5, chunk_order(7)[2 * pair : 2 * pair + 2])
 
         quantise_silu(x_natural, 1)
         for tile in (4, 5):

@@ -275,13 +275,13 @@ def tile_kantlinear_kernel(tc, x, base_weight_words, base_weight_scales, cheby_w
         w_raw[4] = load_w(4)
         prepare_w(4)
 
-        multiply_rows(0, chunk_order(1))
-        multiply_rows(1, chunk_order(2))
+        multiply_rows(0, range(ORDERS))
+        multiply_rows(1, range(ORDERS))
         square(sq_a, t3, 2.0, 0.0)
         for a, b in HALVES:
             shifted_product(sq_c[:, a:b, :], sq_b[:, a:b, :], -2.0, t3[:, a:b, :])
-        multiply_rows(2, chunk_order(3))
-        multiply_rows(3, chunk_order(4))
+        multiply_rows(2, range(ORDERS))
+        multiply_rows(3, range(ORDERS))
 
         x_natural = loads.tile([P, 5120], BF16, name="x_natural", tag="load")
         nc.sync.dma_start(

from contextlib import ExitStack

import concourse.mybir as mybir
from concourse.masks import make_identity

F32 = mybir.dt.float32
BF16 = mybir.dt.bfloat16
I32 = mybir.dt.int32
U32 = mybir.dt.uint32
U8 = mybir.dt.uint8
FP8X4 = mybir.dt.float8_e4m3fn_x4
FP4X4 = mybir.dt.float4_e2m1fn_x4
ALU = mybir.AluOpType
ACT = mybir.ActivationFunctionType

P = 128
ROWS = 1024
FEATURES = 512
OUTS = 512
ORDERS = 10
ROW_TILES = ROWS // P
PASSES = ORDERS + 3
CLASS_ROWS = 104
CLASS_COLS = 4 * CLASS_ROWS
FT_ROWS = 512
FT_COLS = 4 * FT_ROWS + 32
HALVES = ((0, 5), (5, 10))

FLOPS = 2 * ROWS * OUTS * (FEATURES + FEATURES * ORDERS)


def class_runs(order):
    wrap = (ORDERS - 4 * order % ORDERS) % ORDERS
    return [(0, wrap), (wrap, ORDERS - wrap)] if wrap else [(0, ORDERS)]


def chunk_order(order):
    return [(4 * order + rho) % ORDERS for rho in range(ORDERS)]


def tile_kantlinear_kernel(tc, x, base_weight_words, base_weight_scales, cheby_weight, out):
    nc = tc.nc
    with ExitStack() as ctx:
        keep = ctx.enter_context(tc.tile_pool(name="keep", bufs=1))
        loads = ctx.enter_context(tc.tile_pool(name="loads", bufs=3))
        grouped = ctx.enter_context(tc.tile_pool(name="grouped", bufs=3))
        flat_mx = ctx.enter_context(tc.tile_pool(name="flat_mx", bufs=4))
        results = ctx.enter_context(tc.tile_pool(name="results", bufs=3))
        turned = ctx.enter_context(tc.psum_pool(name="turned", bufs=3))
        sums = ctx.enter_context(tc.psum_pool(name="sums", bufs=5))

        w_rows = cheby_weight.rearrange("o i k -> o (i k)")

        def load_w(pair):
            tile = loads.tile([P, 5120], BF16, name="w_raw", tag="load")
            nc.sync.dma_start(
                out=tile[:, 0:4096].rearrange("p (t j) -> p t j", t=4),
                in_=w_rows[:, pair * 1024 : (pair + 1) * 1024].rearrange("(t o) j -> o t j", o=P),
            )
            return tile

        with tc.manual_schedule():
            warm = keep.tile([P, 2], F32, name="warm")
            nc.vector.memset(warm[:, 0:1], 0.0)
            nc.scalar.activation(out=warm[:, 1:2], in_=warm[:, 0:1], func=ACT.Silu)

            ident = keep.tile([P, P], F32, name="ident")
            make_identity(nc, ident[:])

            ft = keep.tile([P, ORDERS, FT_COLS], BF16, name="ft", align_bytes=64)
            nc.gpsimd.memset(ft[:, :, 0:CLASS_COLS], 1.0)

            x_sorted = loads.tile([P, 5120], BF16, name="x_sorted", tag="load")
            ten_rows = "(b r) i -> b (r i)"
            nc.sync.dma_start(out=x_sorted[103:128, :], in_=x[0:250, :].rearrange(ten_rows, r=ORDERS))
            nc.sync.dma_start(out=x_sorted[96:102, :], in_=x[960:1020, :].rearrange(ten_rows, r=ORDERS))
            nc.sync.dma_start(out=x_sorted[102:103, 0:2048], in_=x[1020:1024, :].rearrange(ten_rows, r=4))
            nc.sync.dma_start(out=x_sorted[102:103, 2048:5120], in_=x[0:6, :].rearrange(ten_rows, r=6))
            by_class = x[0:960, :].rearrange("(b r) i -> b r i", r=ORDERS)
            for k in range(5):
                nc.sync.dma_start(
                    out=x_sorted[0:96, k * 1024 : (k + 1) * 1024].rearrange("p (r i) -> p r i", r=2),
                    in_=by_class[:, 2 * k : 2 * k + 2, :],
                )
            w_raw = {0: load_w(0), 1: load_w(1)}

        w4_words = keep.tile([P, 2 * OUTS], U8, name="w4_words", align_bytes=64)
        w4_scales = keep.tile([P, OUTS], U8, name="w4_scales", align_bytes=64)
        nc.vector.memset(w4_scales[:].bitcast(I32), 0)

        xt = keep.tile([P, ORDERS, CLASS_COLS], BF16, name="xt")
        sq_a = keep.tile([P, ORDERS, CLASS_COLS], F32, name="sq_a")
        sq_b = keep.tile([P, ORDERS, CLASS_COLS], F32, name="sq_b")
        sq_c = keep.tile([P, ORDERS, CLASS_COLS], F32, name="sq_c")
        t3 = keep.tile([P, ORDERS, CLASS_COLS], F32, name="t3")

        w_words = keep.tile([P, ORDERS, OUTS], U32, name="w_words", align_bytes=64)
        w_scales = keep.tile([P, ORDERS, OUTS], U8, name="w_scales", align_bytes=64)
        silu_words = keep.tile([P, 2, ROWS], U32, name="silu_words", align_bytes=64)
        silu_scales = keep.tile([P, 2, ROWS], U8, name="silu_scales", align_bytes=64)

        def square(dst, src, scale, bias):
            for a, b in HALVES:
                nc.scalar.activation(out=dst[:, a:b, :], in_=src[:, a:b, :], func=ACT.Square, bias=bias, scale=scale)

        def shifted_product(dst, in0, shift, in1):
            nc.vector.scalar_tensor_tensor(out=dst, in0=in0, scalar=shift, in1=in1, op0=ALU.add, op1=ALU.mult)

        def place(order, first, count):
            s = 4 * order + first
            chunk, row = s % ORDERS, (102 * order + s // ORDERS) % FT_ROWS
            return ft[:, chunk : chunk + count, 4 * row : 4 * row + CLASS_COLS]

        def half_minus_one(engine, order, src, first, count):
            if engine == "vector":
                nc.vector.tensor_scalar(
                    out=place(order, first, count),
                    in0=src[:, first : first + count, :],
                    scalar1=0.5,
                    scalar2=-1.0,
                    op0=ALU.mult,
                    op1=ALU.add,
                )
            else:
                nc.scalar.activation(
                    out=place(order, first, count), in_=src[:, first : first + count, :], func=ACT.Copy, bias=-1.0, scale=0.5
                )

        def prepare_w(pair):
            words = w_raw[pair][:].bitcast(F32)
            for chunk in (2 * pair, 2 * pair + 1):
                w_grouped = grouped.tile([P, 4 * OUTS], BF16, name="w_grouped", tag="grouped", align_bytes=64)
                pairs_out = w_grouped[:].bitcast(F32).rearrange("p (o u) -> p o u", u=2)
                for half in range(2):
                    bank = turned.tile([P, 2, 2 * P], F32, name="w_turned", tag="turned")
                    for block in range(2):
                        for u in range(2):
                            lo = (2 * half + block) * 512 + (chunk % 2) * 256 + u * P
                            nc.tensor.transpose(bank[:, u, block * P : (block + 1) * P], words[:, lo : lo + P], ident[:])
                    nc.scalar.copy(
                        out=pairs_out[:, half * 256 : (half + 1) * 256, :], in_=bank[:].rearrange("p u o -> p o u"))
                nc.vector.quantize_mx(
                    out=w_words[:, chunk, :].bitcast(FP8X4), scales=w_scales[:, chunk, :], in_=w_grouped[:])

        mx = {}
        acc = {}
        passes = {}

        def quantise_rows(tile, chunks):
            if tile not in mx:
                mx[tile] = (
                    flat_mx.tile([P, ORDERS, P], U32, name="flat_words", align_bytes=64),
                    flat_mx.tile([P, ORDERS, P], U8, name="flat_scales", align_bytes=64),
                )
            lo = (tile % 4) * 4 * P
            for c in chunks:
                nc.vector.quantize_mx(
                    out=mx[tile][0][:, c, :].bitcast(FP8X4), scales=mx[tile][1][:, c, :], in_=ft[:, c, lo : lo + 4 * P])

        def one_pass(tile, lhsT, lhsT_scale, rhs, rhs_scale):
            if tile not in acc:
                acc[tile] = sums.tile([P, OUTS], F32, name="acc")
                passes[tile] = 0
            passes[tile] = passes[tile] + 1
            nc.tensor.matmul_mx(
                out=acc[tile][:],
                lhsT=lhsT,
                lhsT_scale=lhsT_scale,
                rhs=rhs,
                rhs_scale=rhs_scale,
                start=(passes[tile] == 1),
                stop=(passes[tile] == PASSES),
            )

        def multiply_rows(tile, chunks):
            for c in chunks:
                one_pass(
                    tile,
                    mx[tile][0][:, c, :].bitcast(FP8X4),
                    mx[tile][1][:, c, :],
                    w_words[:, c, :].bitcast(FP8X4),
                    w_scales[:, c, :],
                )

        def add_base(tile):
            rows = slice(tile * P, (tile + 1) * P)
            for which in (0, 0, 1):
                one_pass(
                    tile,
                    silu_words[:, which, rows].bitcast(FP8X4),
                    silu_scales[:, which, rows],
                    w4_words[:].bitcast(FP4X4),
                    w4_scales[:],
                )

        def finish_rows(tile, engine):
            res = results.tile([P, OUTS], F32, name="res")
            if engine == "vector":
                nc.vector.tensor_scalar(out=res[:], in0=acc[tile][:], scalar1=0.1, scalar2=None, op0=ALU.mult)
            else:
                nc.scalar.mul(out=res[:], in_=acc[tile][:], mul=0.1)
            nc.sync.dma_start(out=out[tile * P : (tile + 1) * P, :], in_=res[:])

        def quantise_silu(x_natural, half):
            words = x_natural[:].bitcast(F32)
            silu = grouped.tile([P, 2048], BF16, name="silu", tag="grouped", align_bytes=64)
            for k in range(2):
                bank = turned.tile([P, 2, 2 * P], F32, name="x_turned", tag="turned")
                for block in range(2):
                    j = 4 * half + 2 * k + block
                    for u in range(2):
                        nc.tensor.transpose(
                            bank[:, u, block * P : (block + 1) * P], words[:, j * 256 + u : (j + 1) * 256 : 2], ident[:])
                nc.scalar.activation(
                    out=silu[:, k * 1024 : (k + 1) * 1024].rearrange("p (q u e) -> p q u e", u=2, e=2),
                    in_=bank[:].bitcast(BF16).rearrange("p u (q e) -> p q u e", e=2),
                    func=ACT.Silu,
                )
            for which in range(2):
                for k in range(2):
                    rows = slice(half * 512 + k * 256, half * 512 + (k + 1) * 256)
                    nc.vector.quantize_mx(
                        out=silu_words[:, which, rows].bitcast(FP8X4),
                        scales=silu_scales[:, which, rows],
                        in_=silu[:, k * 1024 : (k + 1) * 1024],
                    )
                if which == 0:
                    for k in range(2):
                        part = silu[:, k * 1024 : (k + 1) * 1024]
                        nc.vector.tensor_scalar(out=part, in0=part, scalar1=8.0, scalar2=None, op0=ALU.mult)

        sorted_words = x_sorted[:].bitcast(F32)
        xt_words = xt[:].bitcast(F32)
        for k in range(5):
            bank = turned.tile([P, 2, 2, P], F32, name="xs_turned", tag="turned")
            for r in range(2):
                for u in range(2):
                    lo = (2 * k + r) * 256 + u * P
                    nc.tensor.transpose(bank[:, r, u, :], sorted_words[:, lo : lo + P], ident[:])
            nc.vector.tensor_copy(
                out=xt_words[:, 2 * k : 2 * k + 2, :].rearrange("p r (b u) -> p r b u", u=2),
                in_=bank[:, :, :, 0:CLASS_ROWS].rearrange("p r u b -> p r b u"),
            )
            nc.scalar.activation(
                out=sq_a[:, 2 * k : 2 * k + 2, :], in_=xt[:, 2 * k : 2 * k + 2, :], func=ACT.Square, scale=2.0)

        for first, count in class_runs(1):
            nc.vector.tensor_copy(out=place(1, first, count), in_=xt[:, first : first + count, :])
        quantise_rows(0, chunk_order(1))
        prepare_w(0)

        for a, b in HALVES:
            shifted_product(t3[:, a:b, :], sq_a[:, a:b, :], -3.0, xt[:, a:b, :])
        for first, count in class_runs(2):
            half_minus_one("vector", 2, sq_a, first, count)
        quantise_rows(1, chunk_order(2))
        prepare_w(1)

        square(sq_b, sq_a, 1.0, -2.0)
        for first, count in class_runs(3):
            nc.vector.tensor_copy(out=place(3, first, count), in_=t3[:, first : first + count, :])
        quantise_rows(2, chunk_order(3))
        w_raw[2] = load_w(2)
        prepare_w(2)

        square(sq_c, sq_a, 1.0, -2.5)
        for first, count in class_runs(4):
            half_minus_one("vector", 4, sq_b, first, count)
        quantise_rows(3, chunk_order(4))
        w_raw[3] = load_w(3)
        prepare_w(3)

        for first, count in class_runs(5):
            shifted_product(place(5, first, count), sq_c[:, first : first + count, :], -1.25, xt[:, first : first + count, :])
        w_raw[4] = load_w(4)
        prepare_w(4)

        multiply_rows(0, range(ORDERS))
        multiply_rows(1, range(ORDERS))
        square(sq_a, t3, 2.0, 0.0)
        for a, b in HALVES:
            shifted_product(sq_c[:, a:b, :], sq_b[:, a:b, :], -2.0, t3[:, a:b, :])
        multiply_rows(2, range(ORDERS))
        multiply_rows(3, range(ORDERS))

        x_natural = loads.tile([P, 5120], BF16, name="x_natural", tag="load")
        nc.sync.dma_start(
            out=x_natural[:, 0:4096].rearrange("p (j i) -> p j i", j=ROW_TILES), in_=x.rearrange("(j q) i -> q j i", q=P))
        nc.sync.dma_start(out=w4_words[:].bitcast(I32), in_=base_weight_words[0].bitcast(I32))
        for quadrant in range(4):
            nc.sync.dma_start(
                out=w4_scales[32 * quadrant : 32 * quadrant + 4, :].bitcast(I32),
                in_=base_weight_scales[0, 4 * quadrant : 4 * quadrant + 4, :].bitcast(I32),
            )
        quantise_silu(x_natural, 0)
        for tile in range(4):
            add_base(tile)
            finish_rows(tile, "scalar")

        (first_a, count_a), (first_b, count_b) = class_runs(6)
        half_minus_one("scalar", 6, sq_a, first_a, count_a)
        half_minus_one("vector", 6, sq_a, first_b, count_b)
        for pair in range(5):
            quantise_rows(4, chunk_order(6)[2 * pair : 2 * pair + 2])
            multiply_rows(4, chunk_order(6)[2 * pair : 2 * pair + 2])

        for first, count in class_runs(7):
            nc.vector.tensor_tensor(
                out=place(7, first, count),
                in0=sq_c[:, first : first + count, :],
                in1=xt[:, first : first + count, :],
                op=ALU.subtract,
            )
        square(sq_b, sq_b, 1.0, -2.0)
        for pair in range(5):
            quantise_rows(5, chunk_order(7)[2 * pair : 2 * pair + 2])
            multiply_rows(5, chunk_order(7)[2 * pair : 2 * pair + 2])

        quantise_silu(x_natural, 1)
        for tile in (4, 5):
            add_base(tile)
            finish_rows(tile, "scalar")
        add_base(6)
        add_base(7)

        for pair in range(5):
            chunks = (2 * pair, 2 * pair + 1)
            first = (2 * pair - 4 * 8) % ORDERS
            half_minus_one("scalar", 8, sq_b, first, 2)
            first = (2 * pair - 4 * 9) % ORDERS
            shifted_product(place(9, first, 2), sq_a[:, first : first + 2, :], -3.0, t3[:, first : first + 2, :])
            for tile in (6, 7):
                quantise_rows(tile, chunks)
                multiply_rows(tile, chunks)
        finish_rows(6, "scalar")
        finish_rows(7, "vector")
